import numpy as np
import ml_dtypes


def mxq(x, axis, fmt="e4m3"):
    dtype, down = {"e4m3": (ml_dtypes.float8_e4m3fn, 7), "e5m2": (ml_dtypes.float8_e5m2, 14)}[fmt]
    v = np.moveaxis(np.asarray(x, np.float32).astype(ml_dtypes.bfloat16).astype(np.float64), axis, -1)
    blocks = v.reshape(v.shape[:-1] + (-1, 32))
    amax = np.abs(blocks).max(-1, keepdims=True)
    byte = np.maximum(np.where(amax > 0, np.frexp(amax)[1] - 1 + 127, 0) - down, 1)
    scale = np.exp2(byte - 127.0)
    codes = (blocks / scale).astype(np.float32).astype(dtype).astype(np.float64)
    return np.moveaxis((codes * scale).reshape(v.shape), -1, axis)


WIDE = False


def mx_kscale(k):
    if not WIDE:
        return np.ones(k)
    levels = np.array([10, -10, 5, -5, 0])
    a = np.random.permutation(np.resize(levels, k // 512 * 4)).reshape(k // 512, 4)
    idx = np.arange(k)
    return np.exp2(a[idx // 512, idx % 128 // 32])


BF16 = ml_dtypes.bfloat16


def bf(x):
    return np.asarray(x, np.float32).astype(BF16)


def f64(x):
    return np.asarray(x).astype(np.float64)


B, C, H, W, O, KH, KW = 8, 256, 31, 31, 128, 2, 2
K = C * KH * KW
STRIDE = (1, 1)
PAD = (1, 1)
DIL = (1, 1)


def _unfold(x, kh, kw, stride, padding, dilation):
    b, c, h, w = x.shape
    h_out = (h + 2 * padding[0] - dilation[0] * (kh - 1) - 1) // stride[0] + 1
    w_out = (w + 2 * padding[1] - dilation[1] * (kw - 1) - 1) // stride[1] + 1
    xp = np.pad(x, ((0, 0), (0, 0), (padding[0], padding[0]), (padding[1], padding[1])))
    rows = []
    for i in range(kh):
        for j in range(kw):
            r0 = i * dilation[0]
            c0 = j * dilation[1]
            patch = xp[:, :, r0:r0 + h_out * stride[0]:stride[0], c0:c0 + w_out * stride[1]:stride[1]]
            rows.append(patch)
    p = np.stack(rows, axis=1)
    p = p.reshape(b, kh * kw * c, h_out * w_out)
    return p, h_out, w_out


def transform_transposed_unfolded_input(inp_unf):
    return inp_unf


def setup_inputs():
    s = mx_kscale(K)[:C]
    return {"x": bf(np.random.standard_normal((B, C, H, W)) * s[None, :, None, None]),
            "weight": bf(np.random.standard_normal((O, C, KH, KW)) / np.sqrt(K) / s[None, :, None, None]),
            "bias": bf(np.random.standard_normal(O) * 0.5)}


def reference(x, weight, bias):
    x, weight, bias = f64(x), f64(weight), f64(bias)
    b = x.shape[0]
    o = weight.shape[0]
    inp_unf, h_out, w_out = _unfold(x, KH, KW, STRIDE, PAD, DIL)
    inp_t = np.ascontiguousarray(np.swapaxes(inp_unf, 1, 2))
    inp_t = transform_transposed_unfolded_input(inp_t)
    w2d = np.ascontiguousarray(weight.transpose(0, 2, 3, 1)).reshape(o, -1)
    out_lo = mxq(inp_t, 2, "e4m3") @ mxq(w2d, 1, "e4m3").T
    out_unf = np.swapaxes(out_lo, 1, 2)
    out = out_unf.reshape(b, o, h_out, w_out)
    out = out + bias.reshape(1, o, 1, 1)
    return out

@@ -1,0 +1,150 @@
+from contextlib import ExitStack
+
+import concourse.mybir as mybir
+from concourse.masks import make_identity
+
+BF16 = mybir.dt.bfloat16
+F32 = mybir.dt.float32
+I32 = mybir.dt.int32
+U32 = mybir.dt.uint32
+U8 = mybir.dt.uint8
+FP8X4 = mybir.dt.float8_e4m3fn_x4
+IDENT = mybir.ActivationFunctionType.Identity
+
+FLOPS = 2 * 8192 * 1024 * 128
+
+P = 128
+PAIRS = 4
+ROWS = 17
+COLS = ROWS * 64
+ADD = mybir.AluOpType.add
+
+
+def tile_customconvmodule_t_kernel(tc, x, weight, bias, out):
+    nc = tc.nc
+    with ExitStack() as ctx:
+        keep = ctx.enter_context(tc.tile_pool(name="keep", bufs=1))
+        psw = ctx.enter_context(tc.psum_pool(name="psw", bufs=2))
+        psa = ctx.enter_context(tc.psum_pool(name="psa", bufs=3))
+
+        w_sb = keep.tile([P, 1024], BF16, name="w_sb")
+        nc.scalar.dma_start(out=w_sb[:], in_=weight.rearrange("o c i j -> o (c i j)"))
+        b16 = keep.tile([P, 1], BF16, name="b16")
+        with nc.allow_non_contiguous_dma(reason="one bias value a partition"):
+            nc.scalar.dma_start(out=b16[:], in_=bias.rearrange("(o u) -> o u", u=1))
+        xv = x.rearrange("b c h w -> (b c h w)").rearrange("(n q f) -> n q f", n=PAIRS, q=P)
+        raw = []
+        for n in range(PAIRS):
+            r = keep.tile([P, 3844], BF16, name="raw%d" % n)
+            nc.sync.dma_start(out=r[:], in_=xv[n])
+            raw.append(r)
+
+        ident = keep.tile([P, P], F32, name="ident")
+        make_identity(nc, ident[:])
+        w_a = keep.tile([P, 512], U32, name="w_a", align_bytes=64)
+        w_b = keep.tile([P, 512], U32, name="w_b", align_bytes=64)
+        nc.vector.memset(w_a[64:128, :].bitcast(I32), 0)
+        nc.vector.memset(w_b[0:64, :].bitcast(I32), 0)
+        grp = []
+        codes = []
+        planes = []
+        for n in range(PAIRS):
+            g = keep.tile([P, COLS * 4], BF16, name="grp%d" % n, align_bytes=64)
+            gm = g[:].rearrange("q (m e) -> q m e", e=128)
+            nc.vector.memset(gm[:, :, 112:128], 0.0)
+            nc.vector.memset(gm[:, 0, :], 0.0)
+            nc.vector.memset(gm[:, 2 * ROWS - 1, :], 0.0)
+            grp.append(g)
+            codes.append(keep.tile([P, COLS], U32, name="codes%d" % n, align_bytes=64))
+            planes.append(keep.tile([P, COLS], U8, name="planes%d" % n, align_bytes=64))
+
+        b32 = keep.tile([P, 1], F32, name="b32")
+        nc.vector.tensor_copy(out=b32[:], in_=b16[:])
+        w_r = keep.tile([P, 1024], F32, name="w_r")
+        w_src = w_sb[:].bitcast(F32).rearrange("o (p t i) -> o i t p", t=4, i=2)
+        w_dst = w_r[:].rearrange("o (i t g p) -> o i t g p", i=2, t=4, g=2)
+        gw = keep.tile([P, 2048], BF16, name="gw", align_bytes=64)
+        gw_v = gw[:].rearrange("q (i j o t) -> q i j o t", i=2, j=2, t=4)
+        for i in range(2):
+            src = w_src[:, i].unsqueeze(2).to_broadcast([P, 4, 2, 64])
+            if i == 0:
+                nc.vector.tensor_copy(out=w_dst[:, i], in_=src)
+            else:
+                nc.scalar.copy(out=w_dst[:, i], in_=src)
+        for i in range(2):
+            tw = psw.tile([P, 512], F32, name="tw")
+            for t in range(4):
+                nc.tensor.transpose(
+                    tw[:, t * P : (t + 1) * P], w_r[:, (i * 4 + t) * P : (i * 4 + t + 1) * P], ident[:]
+                )
+            src = tw[:].bitcast(BF16).rearrange("q (t o j) -> q j o t", t=4, j=2)
+            if i == 0:
+                nc.vector.tensor_copy(out=gw_v[:, i], in_=src)
+            else:
+                nc.scalar.copy(out=gw_v[:, i], in_=src)
+        w_q = keep.tile([P, 512], U32, name="w_q", align_bytes=64)
+        w_s = keep.tile([P, 512], U8, name="w_s", align_bytes=64)
+        nc.vector.quantize_mx(out=w_q[:].bitcast(FP8X4), scales=w_s[:], in_=gw[:])
+        nc.vector.tensor_copy(out=w_a[0:64, :].bitcast(I32), in_=w_q[0:64, :].bitcast(I32))
+        nc.vector.tensor_copy(out=w_b[64:128, :].bitcast(I32), in_=w_q[64:128, :].bitcast(I32))
+        w_half = [w_a, w_b]
+
+        def regroup(n, s, lo, hi):
+            lo = max(lo, 1) if s == 0 else lo
+            hi = min(hi, 16) if s == 1 else hi
+            src = raw[n][:].rearrange("q (t h w) -> q t h w", t=4, h=31)
+            src = src[:, :, 16 * s + lo - 1 : 16 * s + hi - 1, :].rearrange("q t h w -> q h w t")
+            dst = grp[n][:].rearrange("q (r s w t) -> q r s w t", r=ROWS, s=2, w=32)
+            dst = dst[:, lo:hi, s, 0:31, :]
+            if s == 1:
+                nc.scalar.copy(out=dst, in_=src)
+            else:
+                nc.vector.tensor_copy(out=dst, in_=src)
+
+        def quantise(n, c0, c1):
+            nc.vector.quantize_mx(
+                out=codes[n][:, c0:c1].bitcast(FP8X4),
+                scales=planes[n][:, c0:c1],
+                in_=grp[n][:, 4 * c0 : 4 * c1],
+            )
+
+        res = {}
+
+        def bank(n, g, k):
+            accs = []
+            for j in (1, 0):
+                acc = psa.tile([P, 512], F32, name="acc%d" % j)
+                for i in range(2):
+                    tap = 2 * i + j
+                    c0 = (8 * k + i) * 64
+                    nc.tensor.matmul_mx(
+                        out=acc[:],
+                        lhsT=w_half[g][:, tap * P : (tap + 1) * P].bitcast(FP8X4),
+                        lhsT_scale=w_s[:, tap * P : (tap + 1) * P],
+                        rhs=codes[n][:, c0 : c0 + 512].bitcast(FP8X4),
+                        rhs_scale=planes[n][:, c0 : c0 + 512],
+                        start=(i == 0),
+                        stop=(i == 1),
+                    )
+                accs.append(acc[:].rearrange("o (r s z) -> o s r z", r=8, s=2))
+            if k == 0:
+                res[(n, g)] = keep.tile([P, 1024], F32, name="res%d%d" % (n, g))
+            o_v = res[(n, g)][:].rearrange("o (s r z) -> o s r z", s=2, r=16)[:, :, 8 * k : 8 * k + 8, :]
+            nc.scalar.activation(out=o_v, in_=accs[0], func=IDENT, bias=b32[:, 0:1], scale=1.0)
+            nc.vector.tensor_tensor(
+                out=o_v[:, :, :, 1:32], in0=accs[1][:, :, :, 0:31], in1=o_v[:, :, :, 1:32], op=ADD
+            )
+            if k == 1:
+                nc.sync.dma_start(out=out[2 * n + g].rearrange("o y z -> o (y z)"), in_=res[(n, g)][:])
+
+        for n in range(PAIRS):
+            for s in range(2):
+                regroup(n, s, 0, 9)
+            quantise(n, 0, 512)
+            quantise(n, 512, 576)
+            for s in range(2):
+                regroup(n, s, 9, 17)
+            quantise(n, 576, 1088)
+            for k in range(2):
+                for g in range(2):
+                    bank(n, g, k)

@@ -10,6 +10,7 @@ U32 = mybir.dt.uint32
 U8 = mybir.dt.uint8
 FP8X4 = mybir.dt.float8_e4m3fn_x4
 IDENT = mybir.ActivationFunctionType.Identity
+ADD = mybir.AluOpType.add
 
 FLOPS = 2 * 8192 * 1024 * 128
 
@@ -17,7 +18,6 @@ P = 128
 PAIRS = 4
 ROWS = 17
 COLS = ROWS * 64
-ADD = mybir.AluOpType.add
 
 
 def tile_customconvmodule_t_kernel(tc, x, weight, bias, out):
@@ -26,6 +26,7 @@ def tile_customconvmodule_t_kernel(tc, x, weight, bias, out):
         keep = ctx.enter_context(tc.tile_pool(name="keep", bufs=1))
         psw = ctx.enter_context(tc.psum_pool(name="psw", bufs=2))
         psa = ctx.enter_context(tc.psum_pool(name="psa", bufs=3))
+        ctx.enter_context(tc.manual_schedule())
 
         w_sb = keep.tile([P, 1024], BF16, name="w_sb")
         nc.scalar.dma_start(out=w_sb[:], in_=weight.rearrange("o c i j -> o (c i j)"))
@@ -51,26 +52,40 @@ def tile_customconvmodule_t_kernel(tc, x, weight, bias, out):
         for n in range(PAIRS):
             g = keep.tile([P, COLS * 4], BF16, name="grp%d" % n, align_bytes=64)
             gm = g[:].rearrange("q (m e) -> q m e", e=128)
-            nc.vector.memset(gm[:, :, 112:128], 0.0)
-            nc.vector.memset(gm[:, 0, :], 0.0)
-            nc.vector.memset(gm[:, 2 * ROWS - 1, :], 0.0)
+            eng = nc.vector if n < 2 else nc.gpsimd
+            eng.memset(gm[:, :, 112:128], 0.0)
+            eng.memset(gm[:, 0, :], 0.0)
+            eng.memset(gm[:, 2 * ROWS - 1, :], 0.0)
             grp.append(g)
             codes.append(keep.tile([P, COLS], U32, name="codes%d" % n, align_bytes=64))
             planes.append(keep.tile([P, COLS], U8, name="planes%d" % n, align_bytes=64))
-
         b32 = keep.tile([P, 1], F32, name="b32")
-        nc.vector.tensor_copy(out=b32[:], in_=b16[:])
+        nc.gpsimd.tensor_copy(out=b32[:], in_=b16[:])
+
+        def regroup(eng, n, s, lo, hi):
+            src = raw[n][:].rearrange("q (t h w) -> q t h w", t=4, h=31)
+            src = src[:, :, 16 * s + lo - 1 : 16 * s + hi - 1, :].rearrange("q t h w -> q h w t")
+            dst = grp[n][:].rearrange("q (r s w t) -> q r s w t", r=ROWS, s=2, w=32)
+            dst = dst[:, lo:hi, s, 0:31, :]
+            if eng == 1:
+                nc.scalar.copy(out=dst, in_=src)
+            else:
+                nc.vector.tensor_copy(out=dst, in_=src)
+
+        def quantise(n, c0, c1):
+            nc.vector.quantize_mx(
+                out=codes[n][:, c0:c1].bitcast(FP8X4),
+                scales=planes[n][:, c0:c1],
+                in_=grp[n][:, 4 * c0 : 4 * c1],
+            )
+
         w_r = keep.tile([P, 1024], F32, name="w_r")
         w_src = w_sb[:].bitcast(F32).rearrange("o (p t i) -> o i t p", t=4, i=2)
         w_dst = w_r[:].rearrange("o (i t g p) -> o i t g p", i=2, t=4, g=2)
         gw = keep.tile([P, 2048], BF16, name="gw", align_bytes=64)
         gw_v = gw[:].rearrange("q (i j o t) -> q i j o t", i=2, j=2, t=4)
-        for i in range(2):
-            src = w_src[:, i].unsqueeze(2).to_broadcast([P, 4, 2, 64])
-            if i == 0:
-                nc.vector.tensor_copy(out=w_dst[:, i], in_=src)
-            else:
-                nc.scalar.copy(out=w_dst[:, i], in_=src)
+        nc.vector.tensor_copy(out=w_dst[:, 0], in_=w_src[:, 0].unsqueeze(2).to_broadcast([P, 4, 2, 64]))
+        nc.scalar.copy(out=w_dst[:, 1], in_=w_src[:, 1].unsqueeze(2).to_broadcast([P, 4, 2, 64]))
         for i in range(2):
             tw = psw.tile([P, 512], F32, name="tw")
             for t in range(4):
@@ -84,34 +99,28 @@ def tile_customconvmodule_t_kernel(tc, x, weight, bias, out):
                 nc.scalar.copy(out=gw_v[:, i], in_=src)
         w_q = keep.tile([P, 512], U32, name="w_q", align_bytes=64)
         w_s = keep.tile([P, 512], U8, name="w_s", align_bytes=64)
-        nc.vector.quantize_mx(out=w_q[:].bitcast(FP8X4), scales=w_s[:], in_=gw[:])
-        nc.vector.tensor_copy(out=w_a[0:64, :].bitcast(I32), in_=w_q[0:64, :].bitcast(I32))
-        nc.vector.tensor_copy(out=w_b[64:128, :].bitcast(I32), in_=w_q[64:128, :].bitcast(I32))
         w_half = [w_a, w_b]
 
-        def regroup(n, s, lo, hi):
-            lo = max(lo, 1) if s == 0 else lo
-            hi = min(hi, 16) if s == 1 else hi
-            src = raw[n][:].rearrange("q (t h w) -> q t h w", t=4, h=31)
-            src = src[:, :, 16 * s + lo - 1 : 16 * s + hi - 1, :].rearrange("q t h w -> q h w t")
-            dst = grp[n][:].rearrange("q (r s w t) -> q r s w t", r=ROWS, s=2, w=32)
-            dst = dst[:, lo:hi, s, 0:31, :]
-            if s == 1:
-                nc.scalar.copy(out=dst, in_=src)
-            else:
-                nc.vector.tensor_copy(out=dst, in_=src)
-
-        def quantise(n, c0, c1):
-            nc.vector.quantize_mx(
-                out=codes[n][:, c0:c1].bitcast(FP8X4),
-                scales=planes[n][:, c0:c1],
-                in_=grp[n][:, 4 * c0 : 4 * c1],
-            )
+        regroup(0, 0, 0, 1, 9)
+        regroup(1, 0, 1, 5, 9)
+        regroup(0, 0, 1, 0, 5)
+        nc.vector.quantize_mx(out=w_q[:].bitcast(FP8X4), scales=w_s[:], in_=gw[:])
+        quantise(0, 0, 512)
+        nc.vector.tensor_copy(out=w_a[0:64, :].bitcast(I32), in_=w_q[0:64, :].bitcast(I32))
+        quantise(0, 512, 576)
+        nc.vector.tensor_copy(out=w_b[64:128, :].bitcast(I32), in_=w_q[64:128, :].bitcast(I32))
+        regroup(1, 0, 1, 9, 13)
+        regroup(1, 0, 1, 13, 16)
+        regroup(0, 0, 0, 9, 17)
 
         res = {}
+        accs = {}
 
-        def bank(n, g, k):
-            accs = []
+        def passes(tau):
+            n = tau // 4
+            k = (tau // 2) % 2
+            g = tau % 2
+            views = []
             for j in (1, 0):
                 acc = psa.tile([P, 512], F32, name="acc%d" % j)
                 for i in range(2):
@@ -126,25 +135,58 @@ def tile_customconvmodule_t_kernel(tc, x, weight, bias, out):
                         start=(i == 0),
                         stop=(i == 1),
                     )
-                accs.append(acc[:].rearrange("o (r s z) -> o s r z", r=8, s=2))
+                views.append(acc[:].rearrange("o (r s z) -> o s r z", r=8, s=2))
+            accs[tau] = views
             if k == 0:
                 res[(n, g)] = keep.tile([P, 1024], F32, name="res%d%d" % (n, g))
-            o_v = res[(n, g)][:].rearrange("o (s r z) -> o s r z", s=2, r=16)[:, :, 8 * k : 8 * k + 8, :]
-            nc.scalar.activation(out=o_v, in_=accs[0], func=IDENT, bias=b32[:, 0:1], scale=1.0)
+
+        def out_view(tau):
+            n = tau // 4
+            k = (tau // 2) % 2
+            g = tau % 2
+            return res[(n, g)][:].rearrange("o (s r z) -> o s r z", s=2, r=16)[:, :, 8 * k : 8 * k + 8, :]
+
+        def evacuate(tau):
+            nc.scalar.activation(out=out_view(tau), in_=accs[tau][0], func=IDENT, bias=b32[:, 0:1], scale=1.0)
+
+        def join(tau):
+            n = tau // 4
+            k = (tau // 2) % 2
+            g = tau % 2
+            o_v = out_view(tau)
             nc.vector.tensor_tensor(
-                out=o_v[:, :, :, 1:32], in0=accs[1][:, :, :, 0:31], in1=o_v[:, :, :, 1:32], op=ADD
+                out=o_v[:, :, :, 1:32], in0=accs[tau][1][:, :, :, 0:31], in1=o_v[:, :, :, 1:32], op=ADD
             )
-            if k == 1:
+            dram = out[2 * n + g].rearrange("o (s r) z -> o s r z", s=2)
+            if n == PAIRS - 1:
+                nc.sync.dma_start(out=dram[:, :, 8 * k : 8 * k + 8, :], in_=o_v)
+            elif k == 1:
                 nc.sync.dma_start(out=out[2 * n + g].rearrange("o y z -> o (y z)"), in_=res[(n, g)][:])
 
-        for n in range(PAIRS):
-            for s in range(2):
-                regroup(n, s, 0, 9)
-            quantise(n, 0, 512)
-            quantise(n, 512, 576)
-            for s in range(2):
-                regroup(n, s, 9, 17)
-            quantise(n, 576, 1088)
-            for k in range(2):
-                for g in range(2):
-                    bank(n, g, k)
+        def unit_rows(u):
+            if u % 2 == 0:
+                return (1, 9), (0, 5), (5, 9)
+            return (9, 17), (9, 13), (13, 16)
+
+        for tau in range(16):
+            m = tau // 2
+            passes(tau)
+            evacuate(tau)
+            if tau >= 1:
+                join(tau - 1)
+            if tau % 2 == 0:
+                if m + 1 < 8:
+                    if (m + 1) % 2 == 0:
+                        quantise((m + 1) // 2, 0, 512)
+                        quantise((m + 1) // 2, 512, 576)
+                    else:
+                        quantise((m + 1) // 2, 576, 1088)
+                if m + 2 < 8:
+                    rows = unit_rows(m + 2)
+                    regroup(1, (m + 2) // 2, 1, rows[1][0], rows[1][1])
+            else:
+                if m + 2 < 8:
+                    rows = unit_rows(m + 2)
+                    regroup(0, (m + 2) // 2, 0, rows[0][0], rows[0][1])
+                    regroup(1, (m + 2) // 2, 1, rows[2][0], rows[2][1])
+        join(15)

@@ -25,20 +25,20 @@ def tile_customconvmodule_t_kernel(tc, x, weight, bias, out):
     with ExitStack() as ctx:
         keep = ctx.enter_context(tc.tile_pool(name="keep", bufs=1))
         psw = ctx.enter_context(tc.psum_pool(name="psw", bufs=2))
-        psa = ctx.enter_context(tc.psum_pool(name="psa", bufs=3))
+        psa = ctx.enter_context(tc.psum_pool(name="psa", bufs=6))
         ctx.enter_context(tc.manual_schedule())
 
         w_sb = keep.tile([P, 1024], BF16, name="w_sb")
-        nc.scalar.dma_start(out=w_sb[:], in_=weight.rearrange("o c i j -> o (c i j)"))
-        b16 = keep.tile([P, 1], BF16, name="b16")
-        with nc.allow_non_contiguous_dma(reason="one bias value a partition"):
-            nc.scalar.dma_start(out=b16[:], in_=bias.rearrange("(o u) -> o u", u=1))
+        nc.sync.dma_start(out=w_sb[:], in_=weight.rearrange("o c i j -> o (c i j)"))
         xv = x.rearrange("b c h w -> (b c h w)").rearrange("(n q f) -> n q f", n=PAIRS, q=P)
         raw = []
         for n in range(PAIRS):
             r = keep.tile([P, 3844], BF16, name="raw%d" % n)
             nc.sync.dma_start(out=r[:], in_=xv[n])
             raw.append(r)
+        b16 = keep.tile([P, 1], BF16, name="b16")
+        with nc.allow_non_contiguous_dma(reason="one bias value a partition"):
+            nc.scalar.dma_start(out=b16[:], in_=bias.rearrange("(o u) -> o u", u=1))
 
         ident = keep.tile([P, P], F32, name="ident")
         make_identity(nc, ident[:])
@@ -49,69 +49,111 @@ def tile_customconvmodule_t_kernel(tc, x, weight, bias, out):
         grp = []
         codes = []
         planes = []
+        codes_r = []
+        planes_r = []
         for n in range(PAIRS):
             g = keep.tile([P, COLS * 4], BF16, name="grp%d" % n, align_bytes=64)
-            gm = g[:].rearrange("q (m e) -> q m e", e=128)
-            eng = nc.vector if n < 2 else nc.gpsimd
-            eng.memset(gm[:, :, 112:128], 0.0)
-            eng.memset(gm[:, 0, :], 0.0)
-            eng.memset(gm[:, 2 * ROWS - 1, :], 0.0)
+            gm = g[:].bitcast(I32).rearrange("q (m e) -> q m e", e=64)
+            nc.gpsimd.memset(gm[:, :, 56:64], 0)
+            nc.gpsimd.memset(gm[:, 0, :], 0)
+            nc.gpsimd.memset(gm[:, 2 * ROWS - 1, :], 0)
             grp.append(g)
-            codes.append(keep.tile([P, COLS], U32, name="codes%d" % n, align_bytes=64))
-            planes.append(keep.tile([P, COLS], U8, name="planes%d" % n, align_bytes=64))
+            cd = keep.tile([P, 16 + COLS], U32, name="codes%d" % n, align_bytes=64)
+            nc.gpsimd.memset(cd[:, 0:16].bitcast(I32), 0)
+            pl = keep.tile([P, 64 + COLS], U8, name="planes%d" % n, align_bytes=64)
+            nc.gpsimd.memset(pl[:].bitcast(I32), 0)
+            codes.append(cd)
+            planes.append(pl)
+            codes_r.append(keep.tile([P, COLS], U32, name="codes_r%d" % n, align_bytes=64))
+            planes_r.append(keep.tile([P, COLS], U8, name="planes_r%d" % n, align_bytes=64))
         b32 = keep.tile([P, 1], F32, name="b32")
         nc.gpsimd.tensor_copy(out=b32[:], in_=b16[:])
 
-        def regroup(eng, n, s, lo, hi):
+        def regroup(copy, n, s, lo, hi):
             src = raw[n][:].rearrange("q (t h w) -> q t h w", t=4, h=31)
             src = src[:, :, 16 * s + lo - 1 : 16 * s + hi - 1, :].rearrange("q t h w -> q h w t")
             dst = grp[n][:].rearrange("q (r s w t) -> q r s w t", r=ROWS, s=2, w=32)
-            dst = dst[:, lo:hi, s, 0:31, :]
-            if eng == 1:
-                nc.scalar.copy(out=dst, in_=src)
-            else:
-                nc.vector.tensor_copy(out=dst, in_=src)
+            copy(out=dst[:, lo:hi, s, 0:31, :], in_=src)
 
         def quantise(n, c0, c1):
             nc.vector.quantize_mx(
-                out=codes[n][:, c0:c1].bitcast(FP8X4),
-                scales=planes[n][:, c0:c1],
+                out=codes[n][:, 16 + c0 : 16 + c1].bitcast(FP8X4),
+                scales=planes[n][:, 64 + c0 : 64 + c1],
                 in_=grp[n][:, 4 * c0 : 4 * c1],
             )
+
+        def shift_codes(n, c0, c1):
+            nc.vector.tensor_copy(
+                out=codes_r[n][:, c0:c1].bitcast(I32), in_=codes[n][:, 15 + c0 : 15 + c1].bitcast(I32)
+            )
+
+        def shift_planes(n, c0, c1):
+            nc.vector.tensor_copy(out=planes_r[n][:, c0:c1], in_=planes[n][:, 63 + c0 : 63 + c1])
 
         w_r = keep.tile([P, 1024], F32, name="w_r")
         w_src = w_sb[:].bitcast(F32).rearrange("o (p t i) -> o i t p", t=4, i=2)
         w_dst = w_r[:].rearrange("o (i t g p) -> o i t g p", i=2, t=4, g=2)
-        gw = keep.tile([P, 2048], BF16, name="gw", align_bytes=64)
-        gw_v = gw[:].rearrange("q (i j o t) -> q i j o t", i=2, j=2, t=4)
-        nc.vector.tensor_copy(out=w_dst[:, 0], in_=w_src[:, 0].unsqueeze(2).to_broadcast([P, 4, 2, 64]))
-        nc.scalar.copy(out=w_dst[:, 1], in_=w_src[:, 1].unsqueeze(2).to_broadcast([P, 4, 2, 64]))
+
+        def spread(copy, i, t0, t1):
+            copy(out=w_dst[:, i, t0:t1], in_=w_src[:, i, t0:t1].unsqueeze(2).to_broadcast([P, t1 - t0, 2, 64]))
+
+        spread(nc.vector.tensor_copy, 0, 0, 4)
+        spread(nc.scalar.copy, 1, 2, 4)
+        spread(nc.vector.tensor_copy, 1, 0, 2)
+        tws = []
         for i in range(2):
             tw = psw.tile([P, 512], F32, name="tw")
             for t in range(4):
                 nc.tensor.transpose(
                     tw[:, t * P : (t + 1) * P], w_r[:, (i * 4 + t) * P : (i * 4 + t + 1) * P], ident[:]
                 )
-            src = tw[:].bitcast(BF16).rearrange("q (t o j) -> q j o t", t=4, j=2)
-            if i == 0:
-                nc.vector.tensor_copy(out=gw_v[:, i], in_=src)
-            else:
-                nc.scalar.copy(out=gw_v[:, i], in_=src)
+            tws.append(tw)
+        gw = keep.tile([P, 2048], BF16, name="gw", align_bytes=64)
+        gw_v = gw[:].rearrange("q (j i o t) -> q j i o t", i=2, j=2, t=4)
+
+        def gather_w(copy, i, j):
+            src = tws[i][:].bitcast(BF16).rearrange("q (t o j) -> q j o t", t=4, j=2)
+            copy(out=gw_v[:, j, i], in_=src[:, j])
+
         w_q = keep.tile([P, 512], U32, name="w_q", align_bytes=64)
         w_s = keep.tile([P, 512], U8, name="w_s", align_bytes=64)
         w_half = [w_a, w_b]
 
-        regroup(0, 0, 0, 1, 9)
-        regroup(1, 0, 1, 5, 9)
-        regroup(0, 0, 1, 0, 5)
-        nc.vector.quantize_mx(out=w_q[:].bitcast(FP8X4), scales=w_s[:], in_=gw[:])
+        def quantise_w(j):
+            nc.vector.quantize_mx(
+                out=w_q[:, 256 * j : 256 * j + 256].bitcast(FP8X4),
+                scales=w_s[:, 256 * j : 256 * j + 256],
+                in_=gw[:, 1024 * j : 1024 * j + 1024],
+            )
+
+        def stuff_w(j):
+            for half, lo in ((w_a, 0), (w_b, 64)):
+                nc.vector.tensor_copy(
+                    out=half[lo : lo + 64, 256 * j : 256 * j + 256].bitcast(I32),
+                    in_=w_q[lo : lo + 64, 256 * j : 256 * j + 256].bitcast(I32),
+                )
+
+        vec = nc.vector.tensor_copy
+        act = nc.scalar.copy
+
+        regroup(act, 0, 1, 2, 9)
+        regroup(vec, 0, 0, 1, 9)
+        regroup(vec, 0, 1, 0, 2)
+        gather_w(vec, 0, 1)
+        gather_w(act, 1, 1)
+        gather_w(vec, 0, 0)
+        gather_w(act, 1, 0)
         quantise(0, 0, 512)
-        nc.vector.tensor_copy(out=w_a[0:64, :].bitcast(I32), in_=w_q[0:64, :].bitcast(I32))
+        quantise_w(1)
         quantise(0, 512, 576)
-        nc.vector.tensor_copy(out=w_b[64:128, :].bitcast(I32), in_=w_q[64:128, :].bitcast(I32))
-        regroup(1, 0, 1, 9, 13)
-        regroup(1, 0, 1, 13, 16)
-        regroup(0, 0, 0, 9, 17)
+        stuff_w(1)
+        shift_codes(0, 0, 576)
+        quantise_w(0)
+        shift_planes(0, 0, 576)
+        stuff_w(0)
+        regroup(act, 0, 1, 11, 16)
+        regroup(vec, 0, 0, 9, 17)
+        regroup(vec, 0, 1, 9, 11)
 
         res = {}
         accs = {}
@@ -120,73 +162,73 @@ def tile_customconvmodule_t_kernel(tc, x, weight, bias, out):
             n = tau // 4
             k = (tau // 2) % 2
             g = tau % 2
-            views = []
+            acc = psa.tile([P, 512], F32, name="acc")
             for j in (1, 0):
-                acc = psa.tile([P, 512], F32, name="acc%d" % j)
                 for i in range(2):
-                    tap = 2 * i + j
+                    tap = 2 * j + i
                     c0 = (8 * k + i) * 64
+                    if j == 1:
+                        x_codes = codes[n][:, 16 + c0 : 16 + c0 + 512]
+                        x_plane = planes[n][:, 64 + c0 : 64 + c0 + 512]
+                    else:
+                        x_codes = codes_r[n][:, c0 : c0 + 512]
+                        x_plane = planes_r[n][:, c0 : c0 + 512]
                     nc.tensor.matmul_mx(
                         out=acc[:],
                         lhsT=w_half[g][:, tap * P : (tap + 1) * P].bitcast(FP8X4),
                         lhsT_scale=w_s[:, tap * P : (tap + 1) * P],
-                        rhs=codes[n][:, c0 : c0 + 512].bitcast(FP8X4),
-                        rhs_scale=planes[n][:, c0 : c0 + 512],
-                        start=(i == 0),
-                        stop=(i == 1),
+                        rhs=x_codes.bitcast(FP8X4),
+                        rhs_scale=x_plane,
+                        start=(j == 1 and i == 0),
+                        stop=(j == 0 and i == 1),
                     )
-                views.append(acc[:].rearrange("o (r s z) -> o s r z", r=8, s=2))
-            accs[tau] = views
+            accs[tau] = acc[:].rearrange("o (r s z) -> o s r z", r=8, s=2)
             if k == 0:
                 res[(n, g)] = keep.tile([P, 1024], F32, name="res%d%d" % (n, g))
 
-        def out_view(tau):
+        def evacuate(tau, on_vector=False):
             n = tau // 4
             k = (tau // 2) % 2
             g = tau % 2
-            return res[(n, g)][:].rearrange("o (s r z) -> o s r z", s=2, r=16)[:, :, 8 * k : 8 * k + 8, :]
-
-        def evacuate(tau):
-            nc.scalar.activation(out=out_view(tau), in_=accs[tau][0], func=IDENT, bias=b32[:, 0:1], scale=1.0)
-
-        def join(tau):
-            n = tau // 4
-            k = (tau // 2) % 2
-            g = tau % 2
-            o_v = out_view(tau)
-            nc.vector.tensor_tensor(
-                out=o_v[:, :, :, 1:32], in0=accs[tau][1][:, :, :, 0:31], in1=o_v[:, :, :, 1:32], op=ADD
-            )
+            o_v = res[(n, g)][:].rearrange("o (s r z) -> o s r z", s=2, r=16)[:, :, 8 * k : 8 * k + 8, :]
+            if on_vector:
+                nc.vector.tensor_scalar(out=o_v, in0=accs[tau], scalar1=b32[:, 0:1], scalar2=None, op0=ADD)
+            else:
+                nc.scalar.activation(out=o_v, in_=accs[tau], func=IDENT, bias=b32[:, 0:1], scale=1.0)
             dram = out[2 * n + g].rearrange("o (s r) z -> o s r z", s=2)
             if n == PAIRS - 1:
                 nc.sync.dma_start(out=dram[:, :, 8 * k : 8 * k + 8, :], in_=o_v)
             elif k == 1:
                 nc.sync.dma_start(out=out[2 * n + g].rearrange("o y z -> o (y z)"), in_=res[(n, g)][:])
 
-        def unit_rows(u):
-            if u % 2 == 0:
-                return (1, 9), (0, 5), (5, 9)
-            return (9, 17), (9, 13), (13, 16)
-
-        for tau in range(16):
-            m = tau // 2
-            passes(tau)
-            evacuate(tau)
-            if tau >= 1:
-                join(tau - 1)
-            if tau % 2 == 0:
-                if m + 1 < 8:
-                    if (m + 1) % 2 == 0:
-                        quantise((m + 1) // 2, 0, 512)
-                        quantise((m + 1) // 2, 512, 576)
-                    else:
-                        quantise((m + 1) // 2, 576, 1088)
-                if m + 2 < 8:
-                    rows = unit_rows(m + 2)
-                    regroup(1, (m + 2) // 2, 1, rows[1][0], rows[1][1])
+        def regroup_unit(u):
+            n, k = u // 2, u % 2
+            if k == 0:
+                regroup(act, n, 1, 2, 9)
+                regroup(vec, n, 0, 1, 9)
+                regroup(vec, n, 1, 0, 2)
             else:
-                if m + 2 < 8:
-                    rows = unit_rows(m + 2)
-                    regroup(0, (m + 2) // 2, 0, rows[0][0], rows[0][1])
-                    regroup(1, (m + 2) // 2, 1, rows[2][0], rows[2][1])
-        join(15)
+                regroup(act, n, 1, 11, 16)
+                regroup(vec, n, 0, 9, 17)
+                regroup(vec, n, 1, 9, 11)
+
+        for m in range(8):
+            passes(2 * m)
+            passes(2 * m + 1)
+            n, k = (m + 1) // 2, (m + 1) % 2
+            c0, c1 = ((0, 576), (576, 1088))[k]
+            if m + 1 < 8:
+                if k == 0:
+                    quantise(n, 0, 512)
+                    quantise(n, 512, 576)
+                else:
+                    quantise(n, 576, 1088)
+            if m + 2 < 8:
+                regroup_unit(m + 2)
+            if m + 1 < 8:
+                shift_codes(n, c0, c1)
+                shift_planes(n, c0, c1)
+            if m > 0:
+                evacuate(2 * m - 1)
+            evacuate(2 * m)
+        evacuate(15, on_vector=True)

@@ -87,6 +87,11 @@ def tile_customconvmodule_t_kernel(tc, x, weight, bias, out):
                 out=codes_r[n][:, c0:c1].bitcast(I32), in_=codes[n][:, 15 + c0 : 15 + c1].bitcast(I32)
             )
 
+        def shift_codes_dma(n, c0, c1):
+            nc.sync.dma_start(
+                out=codes_r[n][:, c0:c1].bitcast(I32), in_=codes[n][:, 15 + c0 : 15 + c1].bitcast(I32)
+            )
+
         def shift_planes(n, c0, c1):
             nc.vector.tensor_copy(out=planes_r[n][:, c0:c1], in_=planes[n][:, 63 + c0 : 63 + c1])
 
@@ -151,40 +156,38 @@ def tile_customconvmodule_t_kernel(tc, x, weight, bias, out):
         quantise_w(0)
         shift_planes(0, 0, 576)
         stuff_w(0)
-        regroup(act, 0, 1, 11, 16)
-        regroup(vec, 0, 0, 9, 17)
-        regroup(vec, 0, 1, 9, 11)
-
         res = {}
         accs = {}
 
-        def passes(tau):
-            n = tau // 4
-            k = (tau // 2) % 2
-            g = tau % 2
-            acc = psa.tile([P, 512], F32, name="acc")
+        def passes(u):
+            n, k = u // 2, u % 2
+            pair = []
+            for g in range(2):
+                acc = psa.tile([P, 512], F32, name="acc")
+                pair.append(acc)
+                accs[2 * u + g] = acc[:].rearrange("o (r s z) -> o s r z", r=8, s=2)
+                if k == 0:
+                    res[(n, g)] = keep.tile([P, 1024], F32, name="res%d%d" % (n, g))
             for j in (1, 0):
-                for i in range(2):
-                    tap = 2 * j + i
-                    c0 = (8 * k + i) * 64
-                    if j == 1:
-                        x_codes = codes[n][:, 16 + c0 : 16 + c0 + 512]
-                        x_plane = planes[n][:, 64 + c0 : 64 + c0 + 512]
-                    else:
-                        x_codes = codes_r[n][:, c0 : c0 + 512]
-                        x_plane = planes_r[n][:, c0 : c0 + 512]
-                    nc.tensor.matmul_mx(
-                        out=acc[:],
-                        lhsT=w_half[g][:, tap * P : (tap + 1) * P].bitcast(FP8X4),
-                        lhsT_scale=w_s[:, tap * P : (tap + 1) * P],
-                        rhs=x_codes.bitcast(FP8X4),
-                        rhs_scale=x_plane,
-                        start=(j == 1 and i == 0),
-                        stop=(j == 0 and i == 1),
-                    )
-            accs[tau] = acc[:].rearrange("o (r s z) -> o s r z", r=8, s=2)
-            if k == 0:
-                res[(n, g)] = keep.tile([P, 1024], F32, name="res%d%d" % (n, g))
+                for g in range(2):
+                    for i in range(2):
+                        tap = 2 * j + i
+                        c0 = (8 * k + i) * 64
+                        if j == 1:
+                            x_codes = codes[n][:, 16 + c0 : 16 + c0 + 512]
+                            x_plane = planes[n][:, 64 + c0 : 64 + c0 + 512]
+                        else:
+                            x_codes = codes_r[n][:, c0 : c0 + 512]
+                            x_plane = planes_r[n][:, c0 : c0 + 512]
+                        nc.tensor.matmul_mx(
+                            out=pair[g][:],
+                            lhsT=w_half[g][:, tap * P : (tap + 1) * P].bitcast(FP8X4),
+                            lhsT_scale=w_s[:, tap * P : (tap + 1) * P],
+                            rhs=x_codes.bitcast(FP8X4),
+                            rhs_scale=x_plane,
+                            start=(j == 1 and i == 0),
+                            stop=(j == 0 and i == 1),
+                        )
 
         def evacuate(tau, on_vector=False):
             n = tau // 4
@@ -202,32 +205,48 @@ def tile_customconvmodule_t_kernel(tc, x, weight, bias, out):
                 nc.sync.dma_start(out=out[2 * n + g].rearrange("o y z -> o (y z)"), in_=res[(n, g)][:])
 
         def regroup_unit(u):
+            if u > 7:
+                return
             n, k = u // 2, u % 2
             if k == 0:
-                regroup(act, n, 1, 2, 9)
+                regroup(act, n, 1, 4, 9)
                 regroup(vec, n, 0, 1, 9)
-                regroup(vec, n, 1, 0, 2)
+                regroup(vec, n, 1, 0, 4)
             else:
                 regroup(act, n, 1, 11, 16)
                 regroup(vec, n, 0, 9, 17)
                 regroup(vec, n, 1, 9, 11)
 
+        def quantise_unit(u):
+            if u > 7:
+                return
+            n, k = u // 2, u % 2
+            if k == 0:
+                quantise(n, 0, 512)
+                quantise(n, 512, 576)
+            else:
+                quantise(n, 576, 1088)
+            if u < 7:
+                shift_codes_dma(n, 576 * k, 576 + 512 * k)
+
+        def shift_unit(u):
+            if u > 7:
+                return
+            n, k = u // 2, u % 2
+            shift_planes(n, 576 * k, 576 + 512 * k)
+            if u == 7:
+                shift_codes(n, 576 * k, 576 + 512 * k)
+
+        regroup_unit(1)
+        regroup_unit(2)
+        quantise_unit(1)
         for m in range(8):
-            passes(2 * m)
-            passes(2 * m + 1)
-            n, k = (m + 1) // 2, (m + 1) % 2
-            c0, c1 = ((0, 576), (576, 1088))[k]
-            if m + 1 < 8:
-                if k == 0:
-                    quantise(n, 0, 512)
-                    quantise(n, 512, 576)
-                else:
-                    quantise(n, 576, 1088)
-            if m + 2 < 8:
-                regroup_unit(m + 2)
-            if m + 1 < 8:
-                shift_codes(n, c0, c1)
-                shift_planes(n, c0, c1)
+            passes(m)
+            if m == 0:
+                shift_unit(1)
+            quantise_unit(m + 2)
+            regroup_unit(m + 3)
+            shift_unit(m + 2)
             if m > 0:
                 evacuate(2 * m - 1)
             evacuate(2 * m)

@@ -18,29 +18,31 @@ P = 128
 PAIRS = 4
 ROWS = 17
 COLS = ROWS * 64
+UNITS = ((0, 0, 8), (0, 8, 16), (1, 0, 8), (1, 8, 16), (2, 0, 8), (2, 8, 16), (3, 0, 8), (3, 8, 12), (3, 12, 16))
+LAST = len(UNITS) - 1
 
 
 def tile_customconvmodule_t_kernel(tc, x, weight, bias, out):
     nc = tc.nc
     with ExitStack() as ctx:
         keep = ctx.enter_context(tc.tile_pool(name="keep", bufs=1))
-        psw = ctx.enter_context(tc.psum_pool(name="psw", bufs=2))
-        psa = ctx.enter_context(tc.psum_pool(name="psa", bufs=6))
+        psw = ctx.enter_context(tc.psum_pool(name="psw", bufs=4))
+        psa = ctx.enter_context(tc.psum_pool(name="psa", bufs=4))
         ctx.enter_context(tc.manual_schedule())
 
-        w_sb = keep.tile([P, 1024], BF16, name="w_sb")
-        nc.sync.dma_start(out=w_sb[:], in_=weight.rearrange("o c i j -> o (c i j)"))
+        b16 = keep.tile([P, 1], BF16, name="b16")
+        with nc.allow_non_contiguous_dma(reason="one bias value a partition"):
+            nc.scalar.dma_start(out=b16[:], in_=bias.rearrange("(o u) -> o u", u=1))
+        w_sb = keep.tile([P, 2048], BF16, name="w_sb")
+        nc.sync.dma_start(out=w_sb[:, 0:1024], in_=weight.rearrange("o c i j -> o (c i j)"))
         xv = x.rearrange("b c h w -> (b c h w)").rearrange("(n q f) -> n q f", n=PAIRS, q=P)
         raw = []
         for n in range(PAIRS):
             r = keep.tile([P, 3844], BF16, name="raw%d" % n)
-            nc.sync.dma_start(out=r[:], in_=xv[n])
             raw.append(r)
-        b16 = keep.tile([P, 1], BF16, name="b16")
-        with nc.allow_non_contiguous_dma(reason="one bias value a partition"):
-            nc.scalar.dma_start(out=b16[:], in_=bias.rearrange("(o u) -> o u", u=1))
+            nc.sync.dma_start(out=r[:], in_=xv[n])
 
-        ident = keep.tile([P, P], F32, name="ident")
+        ident = keep.tile([P, P], BF16, name="ident")
         make_identity(nc, ident[:])
         w_a = keep.tile([P, 512], U32, name="w_a", align_bytes=64)
         w_b = keep.tile([P, 512], U32, name="w_b", align_bytes=64)
@@ -67,7 +69,6 @@ def tile_customconvmodule_t_kernel(tc, x, weight, bias, out):
             codes_r.append(keep.tile([P, COLS], U32, name="codes_r%d" % n, align_bytes=64))
             planes_r.append(keep.tile([P, COLS], U8, name="planes_r%d" % n, align_bytes=64))
         b32 = keep.tile([P, 1], F32, name="b32")
-        nc.gpsimd.tensor_copy(out=b32[:], in_=b16[:])
 
         def regroup(copy, n, s, lo, hi):
             src = raw[n][:].rearrange("q (t h w) -> q t h w", t=4, h=31)
@@ -75,50 +76,21 @@ def tile_customconvmodule_t_kernel(tc, x, weight, bias, out):
             dst = grp[n][:].rearrange("q (r s w t) -> q r s w t", r=ROWS, s=2, w=32)
             copy(out=dst[:, lo:hi, s, 0:31, :], in_=src)
 
-        def quantise(n, c0, c1):
-            nc.vector.quantize_mx(
-                out=codes[n][:, 16 + c0 : 16 + c1].bitcast(FP8X4),
-                scales=planes[n][:, 64 + c0 : 64 + c1],
-                in_=grp[n][:, 4 * c0 : 4 * c1],
-            )
+        tws = {}
 
-        def shift_codes(n, c0, c1):
-            nc.vector.tensor_copy(
-                out=codes_r[n][:, c0:c1].bitcast(I32), in_=codes[n][:, 15 + c0 : 15 + c1].bitcast(I32)
-            )
-
-        def shift_codes_dma(n, c0, c1):
-            nc.sync.dma_start(
-                out=codes_r[n][:, c0:c1].bitcast(I32), in_=codes[n][:, 15 + c0 : 15 + c1].bitcast(I32)
-            )
-
-        def shift_planes(n, c0, c1):
-            nc.vector.tensor_copy(out=planes_r[n][:, c0:c1], in_=planes[n][:, 63 + c0 : 63 + c1])
-
-        w_r = keep.tile([P, 1024], F32, name="w_r")
-        w_src = w_sb[:].bitcast(F32).rearrange("o (p t i) -> o i t p", t=4, i=2)
-        w_dst = w_r[:].rearrange("o (i t g p) -> o i t g p", i=2, t=4, g=2)
-
-        def spread(copy, i, t0, t1):
-            copy(out=w_dst[:, i, t0:t1], in_=w_src[:, i, t0:t1].unsqueeze(2).to_broadcast([P, t1 - t0, 2, 64]))
-
-        spread(nc.vector.tensor_copy, 0, 0, 4)
-        spread(nc.scalar.copy, 1, 2, 4)
-        spread(nc.vector.tensor_copy, 1, 0, 2)
-        tws = []
-        for i in range(2):
+        def turn_w(i, j):
             tw = psw.tile([P, 512], F32, name="tw")
+            view = tw[:].rearrange("q (o t) -> q o t", t=4)
             for t in range(4):
-                nc.tensor.transpose(
-                    tw[:, t * P : (t + 1) * P], w_r[:, (i * 4 + t) * P : (i * 4 + t + 1) * P], ident[:]
-                )
-            tws.append(tw)
+                first = 4 * t + 2 * i + j
+                nc.tensor.matmul(view[:, :, t], lhsT=w_sb[:, first : 2048 : 16], rhs=ident[:], start=True, stop=True)
+            tws[(i, j)] = tw
+
         gw = keep.tile([P, 2048], BF16, name="gw", align_bytes=64)
-        gw_v = gw[:].rearrange("q (j i o t) -> q j i o t", i=2, j=2, t=4)
 
         def gather_w(copy, i, j):
-            src = tws[i][:].bitcast(BF16).rearrange("q (t o j) -> q j o t", t=4, j=2)
-            copy(out=gw_v[:, j, i], in_=src[:, j])
+            c0 = 1024 * j + 512 * i
+            copy(out=gw[:, c0 : c0 + 512], in_=tws[(i, j)][:])
 
         w_q = keep.tile([P, 512], U32, name="w_q", align_bytes=64)
         w_s = keep.tile([P, 512], U8, name="w_s", align_bytes=64)
@@ -141,113 +113,142 @@ def tile_customconvmodule_t_kernel(tc, x, weight, bias, out):
         vec = nc.vector.tensor_copy
         act = nc.scalar.copy
 
-        regroup(act, 0, 1, 2, 9)
-        regroup(vec, 0, 0, 1, 9)
-        regroup(vec, 0, 1, 0, 2)
-        gather_w(vec, 0, 1)
-        gather_w(act, 1, 1)
-        gather_w(vec, 0, 0)
-        gather_w(act, 1, 0)
-        quantise(0, 0, 512)
-        quantise_w(1)
-        quantise(0, 512, 576)
-        stuff_w(1)
-        shift_codes(0, 0, 576)
-        quantise_w(0)
-        shift_planes(0, 0, 576)
-        stuff_w(0)
+        def columns(u):
+            n, lo, hi = UNITS[u]
+            return (0 if lo == 0 else 64 * (lo + 1)), 64 * (hi + 1)
+
+        def quantise(u, part=None):
+            n = UNITS[u][0]
+            c0, c1 = columns(u)
+            pieces = [(c0, c1)] if c0 else [(0, c1 - 64), (c1 - 64, c1)]
+            for a, b in pieces if part is None else [pieces[part]]:
+                nc.vector.quantize_mx(
+                    out=codes[n][:, 16 + a : 16 + b].bitcast(FP8X4),
+                    scales=planes[n][:, 64 + a : 64 + b],
+                    in_=grp[n][:, 4 * a : 4 * b],
+                )
+
+        def shift_codes(u, queue=None):
+            n = UNITS[u][0]
+            c0, c1 = columns(u)
+            move = nc.vector.tensor_copy if queue is None else queue.dma_start
+            move(out=codes_r[n][:, c0:c1].bitcast(I32), in_=codes[n][:, 15 + c0 : 15 + c1].bitcast(I32))
+
+        def shift_planes(u):
+            n = UNITS[u][0]
+            c0, c1 = columns(u)
+            nc.vector.tensor_copy(out=planes_r[n][:, c0:c1], in_=planes[n][:, 63 + c0 : 63 + c1])
+
         res = {}
+        for n in range(PAIRS):
+            for g in range(2):
+                res[(n, g)] = keep.tile([P, 1024], F32, name="res%d%d" % (n, g))
         accs = {}
 
-        def passes(u):
-            n, k = u // 2, u % 2
-            pair = []
-            for g in range(2):
-                acc = psa.tile([P, 512], F32, name="acc")
-                pair.append(acc)
-                accs[2 * u + g] = acc[:].rearrange("o (r s z) -> o s r z", r=8, s=2)
-                if k == 0:
-                    res[(n, g)] = keep.tile([P, 1024], F32, name="res%d%d" % (n, g))
-            for j in (1, 0):
-                for g in range(2):
-                    for i in range(2):
-                        tap = 2 * j + i
-                        c0 = (8 * k + i) * 64
-                        if j == 1:
-                            x_codes = codes[n][:, 16 + c0 : 16 + c0 + 512]
-                            x_plane = planes[n][:, 64 + c0 : 64 + c0 + 512]
-                        else:
-                            x_codes = codes_r[n][:, c0 : c0 + 512]
-                            x_plane = planes_r[n][:, c0 : c0 + 512]
-                        nc.tensor.matmul_mx(
-                            out=pair[g][:],
-                            lhsT=w_half[g][:, tap * P : (tap + 1) * P].bitcast(FP8X4),
-                            lhsT_scale=w_s[:, tap * P : (tap + 1) * P],
-                            rhs=x_codes.bitcast(FP8X4),
-                            rhs_scale=x_plane,
-                            start=(j == 1 and i == 0),
-                            stop=(j == 0 and i == 1),
-                        )
+        def passes(u, order):
+            n, lo, hi = UNITS[u]
+            width = 64 * (hi - lo)
+            for j, g in order:
+                if j == 1:
+                    acc = psa.tile([P, 512], F32, name="acc")
+                    accs[(u, g)] = acc
+                acc = accs[(u, g)]
+                for i in range(2):
+                    tap = 2 * j + i
+                    c0 = (lo + i) * 64
+                    if j == 1:
+                        x_codes = codes[n][:, 16 + c0 : 16 + c0 + width]
+                        x_plane = planes[n][:, 64 + c0 : 64 + c0 + width]
+                    else:
+                        x_codes = codes_r[n][:, c0 : c0 + width]
+                        x_plane = planes_r[n][:, c0 : c0 + width]
+                    nc.tensor.matmul_mx(
+                        out=acc[:, 0:width],
+                        lhsT=w_half[g][:, tap * P : (tap + 1) * P].bitcast(FP8X4),
+                        lhsT_scale=w_s[:, tap * P : (tap + 1) * P],
+                        rhs=x_codes.bitcast(FP8X4),
+                        rhs_scale=x_plane,
+                        start=(j == 1 and i == 0),
+                        stop=(j == 0 and i == 1),
+                    )
 
-        def evacuate(tau, on_vector=False):
-            n = tau // 4
-            k = (tau // 2) % 2
-            g = tau % 2
-            o_v = res[(n, g)][:].rearrange("o (s r z) -> o s r z", s=2, r=16)[:, :, 8 * k : 8 * k + 8, :]
+        def evacuate(u, g, on_vector=False):
+            n, lo, hi = UNITS[u]
+            src = accs[(u, g)][:, 0 : 64 * (hi - lo)].rearrange("o (r s z) -> o s r z", s=2, z=32)
+            o_v = res[(n, g)][:].rearrange("o (s r z) -> o s r z", s=2, r=16)[:, :, lo:hi, :]
             if on_vector:
-                nc.vector.tensor_scalar(out=o_v, in0=accs[tau], scalar1=b32[:, 0:1], scalar2=None, op0=ADD)
+                nc.vector.tensor_scalar(out=o_v, in0=src, scalar1=b32[:, 0:1], scalar2=None, op0=ADD)
             else:
-                nc.scalar.activation(out=o_v, in_=accs[tau], func=IDENT, bias=b32[:, 0:1], scale=1.0)
-            dram = out[2 * n + g].rearrange("o (s r) z -> o s r z", s=2)
+                nc.scalar.activation(out=o_v, in_=src, func=IDENT, bias=b32[:, 0:1], scale=1.0)
+
+        def store(u, g):
+            n, lo, hi = UNITS[u]
             if n == PAIRS - 1:
-                nc.sync.dma_start(out=dram[:, :, 8 * k : 8 * k + 8, :], in_=o_v)
-            elif k == 1:
+                dram = out[2 * n + g].rearrange("o (s r) z -> o s r z", s=2)
+                o_v = res[(n, g)][:].rearrange("o (s r z) -> o s r z", s=2, r=16)
+                nc.sync.dma_start(out=dram[:, :, lo:hi, :], in_=o_v[:, :, lo:hi, :])
+            elif hi == 16:
                 nc.sync.dma_start(out=out[2 * n + g].rearrange("o y z -> o (y z)"), in_=res[(n, g)][:])
 
+        both = ((1, 0), (1, 1), (0, 0), (0, 1))
+        in_turn = ((1, 0), (0, 0), (1, 1), (0, 1))
+
+        shares = (
+            ((act, 1, 2, 9), (vec, 0, 1, 9), (vec, 1, 0, 2)),
+            ((act, 1, 9, 16), (act, 0, 13, 17), (vec, 0, 9, 13)),
+            ((act, 1, 2, 9), (vec, 0, 1, 9), (vec, 1, 0, 2)),
+            ((act, 1, 11, 16), (vec, 0, 9, 17), (vec, 1, 9, 11)),
+            ((act, 1, 2, 9), (vec, 0, 1, 9), (vec, 1, 0, 2)),
+            ((act, 1, 11, 16), (vec, 0, 9, 17), (vec, 1, 9, 11)),
+            ((act, 1, 2, 9), (vec, 0, 1, 9), (vec, 1, 0, 2)),
+            ((act, 1, 11, 13), (vec, 0, 9, 13), (vec, 1, 9, 11)),
+            ((act, 1, 13, 16), (vec, 0, 13, 17)),
+        )
+
         def regroup_unit(u):
-            if u > 7:
-                return
-            n, k = u // 2, u % 2
-            if k == 0:
-                regroup(act, n, 1, 4, 9)
-                regroup(vec, n, 0, 1, 9)
-                regroup(vec, n, 1, 0, 4)
-            else:
-                regroup(act, n, 1, 11, 16)
-                regroup(vec, n, 0, 9, 17)
-                regroup(vec, n, 1, 9, 11)
+            for copy, s, lo, hi in shares[u]:
+                regroup(copy, UNITS[u][0], s, lo, hi)
 
-        def quantise_unit(u):
-            if u > 7:
-                return
-            n, k = u // 2, u % 2
-            if k == 0:
-                quantise(n, 0, 512)
-                quantise(n, 512, 576)
-            else:
-                quantise(n, 576, 1088)
-            if u < 7:
-                shift_codes_dma(n, 576 * k, 576 + 512 * k)
-
-        def shift_unit(u):
-            if u > 7:
-                return
-            n, k = u // 2, u % 2
-            shift_planes(n, 576 * k, 576 + 512 * k)
-            if u == 7:
-                shift_codes(n, 576 * k, 576 + 512 * k)
-
+        vec(out=w_sb[:, 1024:2048], in_=w_sb[:, 0:1024])
+        turn_w(0, 1)
+        turn_w(1, 1)
+        turn_w(0, 0)
+        turn_w(1, 0)
+        gather_w(act, 0, 1)
+        regroup_unit(0)
+        gather_w(vec, 1, 1)
+        gather_w(act, 0, 0)
+        gather_w(act, 1, 0)
+        act(out=b32[:], in_=b16[:])
+        quantise_w(1)
+        quantise(0)
+        stuff_w(1)
+        quantise_w(0)
+        shift_codes(0)
+        shift_planes(0)
+        stuff_w(0)
         regroup_unit(1)
+        quantise(1)
         regroup_unit(2)
-        quantise_unit(1)
-        for m in range(8):
-            passes(m)
-            if m == 0:
-                shift_unit(1)
-            quantise_unit(m + 2)
-            regroup_unit(m + 3)
-            shift_unit(m + 2)
-            if m > 0:
-                evacuate(2 * m - 1)
-            evacuate(2 * m)
-        evacuate(15, on_vector=True)
+        shift_codes(1)
+        shift_planes(1)
+        by_dma = (3, 4, 5, 6)
+        for u in range(LAST + 1):
+            passes(u, both if u < LAST else in_turn)
+            if u + 2 <= LAST:
+                quantise(u + 2)
+                if u + 2 in by_dma:
+                    shift_codes(u + 2, nc.sync)
+            if u + 3 <= LAST:
+                regroup_unit(u + 3)
+            if u + 2 <= LAST:
+                if u + 2 not in by_dma:
+                    shift_codes(u + 2)
+                shift_planes(u + 2)
+            if u > 0:
+                evacuate(u - 1, 1)
+                store(u - 1, 1)
+            evacuate(u, 0)
+            store(u, 0)
+        evacuate(LAST, 1, on_vector=True)
+        store(LAST, 1)

@@ -30,9 +30,9 @@ def tile_customconvmodule_t_kernel(tc, x, weight, bias, out):
         psa = ctx.enter_context(tc.psum_pool(name="psa", bufs=4))
         ctx.enter_context(tc.manual_schedule())
 
-        b16 = keep.tile([P, 1], BF16, name="b16")
-        with nc.allow_non_contiguous_dma(reason="one bias value a partition"):
-            nc.scalar.dma_start(out=b16[:], in_=bias.rearrange("(o u) -> o u", u=1))
+        b_row = keep.tile([P, P], BF16, name="b_row")
+        nc.vector.memset(b_row[:].bitcast(I32), 0)
+        nc.scalar.dma_start(out=b_row[0:1, :], in_=bias.rearrange("(u o) -> u o", u=1))
         w_sb = keep.tile([P, 2048], BF16, name="w_sb")
         nc.sync.dma_start(out=w_sb[:, 0:1024], in_=weight.rearrange("o c i j -> o (c i j)"))
         xv = x.rearrange("b c h w -> (b c h w)").rearrange("(n q f) -> n q f", n=PAIRS, q=P)
@@ -46,34 +46,31 @@ def tile_customconvmodule_t_kernel(tc, x, weight, bias, out):
         make_identity(nc, ident[:])
         w_a = keep.tile([P, 512], U32, name="w_a", align_bytes=64)
         w_b = keep.tile([P, 512], U32, name="w_b", align_bytes=64)
+        grp_all = keep.tile([P, PAIRS, COLS * 4], BF16, name="grp", align_bytes=64)
+        codes_all = keep.tile([P, PAIRS, 16 + COLS], U32, name="codes", align_bytes=64)
+        planes_all = keep.tile([P, PAIRS, 64 + COLS], U8, name="planes", align_bytes=64)
+        codes_r_all = keep.tile([P, PAIRS, COLS], U32, name="codes_r", align_bytes=64)
+        planes_r_all = keep.tile([P, PAIRS, COLS], U8, name="planes_r", align_bytes=64)
+        grp = [grp_all[:, n, :] for n in range(PAIRS)]
+        codes = [codes_all[:, n, :] for n in range(PAIRS)]
+        planes = [planes_all[:, n, :] for n in range(PAIRS)]
+        codes_r = [codes_r_all[:, n, :] for n in range(PAIRS)]
+        planes_r = [planes_r_all[:, n, :] for n in range(PAIRS)]
+        gm = grp_all[:].bitcast(I32).rearrange("q n (m e) -> q n m e", e=64)
+        nc.vector.memset(gm[:, :, :, 56:64], 0)
+        nc.vector.memset(gm[:, :, 0, 0:56], 0)
+        nc.vector.memset(gm[:, :, 2 * ROWS - 1, 0:56], 0)
+        nc.vector.memset(codes_all[:, :, 0:16].bitcast(I32), 0)
+        nc.vector.memset(planes_all[:].bitcast(I32), 0)
         nc.vector.memset(w_a[64:128, :].bitcast(I32), 0)
         nc.vector.memset(w_b[0:64, :].bitcast(I32), 0)
-        grp = []
-        codes = []
-        planes = []
-        codes_r = []
-        planes_r = []
-        for n in range(PAIRS):
-            g = keep.tile([P, COLS * 4], BF16, name="grp%d" % n, align_bytes=64)
-            gm = g[:].bitcast(I32).rearrange("q (m e) -> q m e", e=64)
-            nc.gpsimd.memset(gm[:, :, 56:64], 0)
-            nc.gpsimd.memset(gm[:, 0, :], 0)
-            nc.gpsimd.memset(gm[:, 2 * ROWS - 1, :], 0)
-            grp.append(g)
-            cd = keep.tile([P, 16 + COLS], U32, name="codes%d" % n, align_bytes=64)
-            nc.gpsimd.memset(cd[:, 0:16].bitcast(I32), 0)
-            pl = keep.tile([P, 64 + COLS], U8, name="planes%d" % n, align_bytes=64)
-            nc.gpsimd.memset(pl[:].bitcast(I32), 0)
-            codes.append(cd)
-            planes.append(pl)
-            codes_r.append(keep.tile([P, COLS], U32, name="codes_r%d" % n, align_bytes=64))
-            planes_r.append(keep.tile([P, COLS], U8, name="planes_r%d" % n, align_bytes=64))
         b32 = keep.tile([P, 1], F32, name="b32")
+        b_col = psa.tile([P, 512], F32, name="acc")
 
         def regroup(copy, n, s, lo, hi):
             src = raw[n][:].rearrange("q (t h w) -> q t h w", t=4, h=31)
             src = src[:, :, 16 * s + lo - 1 : 16 * s + hi - 1, :].rearrange("q t h w -> q h w t")
-            dst = grp[n][:].rearrange("q (r s w t) -> q r s w t", r=ROWS, s=2, w=32)
+            dst = grp[n].rearrange("q (r s w t) -> q r s w t", r=ROWS, s=2, w=32)
             copy(out=dst[:, lo:hi, s, 0:31, :], in_=src)
 
         tws = {}
@@ -219,7 +216,8 @@ def tile_customconvmodule_t_kernel(tc, x, weight, bias, out):
         gather_w(vec, 1, 1)
         gather_w(act, 0, 0)
         gather_w(act, 1, 0)
-        act(out=b32[:], in_=b16[:])
+        nc.tensor.matmul(b_col[:, 0:1], lhsT=b_row[:], rhs=ident[:, 0:1], start=True, stop=True)
+        act(out=b32[:], in_=b_col[:, 0:1])
         quantise_w(1)
         quantise(0)
         stuff_w(1)

@@ -58,14 +58,9 @@ def tile_customconvmodule_t_kernel(tc, x, weight, bias, out):
         planes_r = [planes_r_all[:, n, :] for n in range(PAIRS)]
         gm = grp_all[:].bitcast(I32).rearrange("q n (m e) -> q n m e", e=64)
         nc.vector.memset(gm[:, :, :, 56:64], 0)
-        nc.vector.memset(gm[:, :, 0, 0:56], 0)
-        nc.vector.memset(gm[:, :, 2 * ROWS - 1, 0:56], 0)
-        nc.vector.memset(codes_all[:, :, 0:16].bitcast(I32), 0)
-        nc.vector.memset(planes_all[:].bitcast(I32), 0)
         nc.vector.memset(w_a[64:128, :].bitcast(I32), 0)
         nc.vector.memset(w_b[0:64, :].bitcast(I32), 0)
         b32 = keep.tile([P, 1], F32, name="b32")
-        b_col = psa.tile([P, 512], F32, name="acc")
 
         def regroup(copy, n, s, lo, hi):
             src = raw[n][:].rearrange("q (t h w) -> q t h w", t=4, h=31)
@@ -207,6 +202,10 @@ def tile_customconvmodule_t_kernel(tc, x, weight, bias, out):
                 regroup(copy, UNITS[u][0], s, lo, hi)
 
         vec(out=w_sb[:, 1024:2048], in_=w_sb[:, 0:1024])
+        nc.vector.memset(gm[:, :, 0, 0:56], 0)
+        nc.vector.memset(gm[:, :, 2 * ROWS - 1, 0:56], 0)
+        nc.vector.memset(codes_all[:, :, 0:16].bitcast(I32), 0)
+        nc.vector.memset(planes_all[:].bitcast(I32), 0)
         turn_w(0, 1)
         turn_w(1, 1)
         turn_w(0, 0)
@@ -216,8 +215,6 @@ def tile_customconvmodule_t_kernel(tc, x, weight, bias, out):
         gather_w(vec, 1, 1)
         gather_w(act, 0, 0)
         gather_w(act, 1, 0)
-        nc.tensor.matmul(b_col[:, 0:1], lhsT=b_row[:], rhs=ident[:, 0:1], start=True, stop=True)
-        act(out=b32[:], in_=b_col[:, 0:1])
         quantise_w(1)
         quantise(0)
         stuff_w(1)
@@ -233,6 +230,10 @@ def tile_customconvmodule_t_kernel(tc, x, weight, bias, out):
         by_dma = (3, 4, 5, 6)
         for u in range(LAST + 1):
             passes(u, both if u < LAST else in_turn)
+            if u == 0:
+                b_col = psw.tile([P, 512], F32, name="tw")
+                nc.tensor.matmul(b_col[:, 0:1], lhsT=b_row[:], rhs=ident[:, 0:1], start=True, stop=True)
+                act(out=b32[:], in_=b_col[:, 0:1])
             if u + 2 <= LAST:
                 quantise(u + 2)
                 if u + 2 in by_dma:

@@ -26,12 +26,11 @@ def tile_customconvmodule_t_kernel(tc, x, weight, bias, out):
     nc = tc.nc
     with ExitStack() as ctx:
         keep = ctx.enter_context(tc.tile_pool(name="keep", bufs=1))
-        psw = ctx.enter_context(tc.psum_pool(name="psw", bufs=4))
-        psa = ctx.enter_context(tc.psum_pool(name="psa", bufs=4))
+        psum = ctx.enter_context(tc.psum_pool(name="psum", bufs=8))
         ctx.enter_context(tc.manual_schedule())
 
         b_row = keep.tile([P, P], BF16, name="b_row")
-        nc.vector.memset(b_row[:].bitcast(I32), 0)
+        nc.gpsimd.memset(b_row[:].bitcast(I32), 0)
         nc.scalar.dma_start(out=b_row[0:1, :], in_=bias.rearrange("(u o) -> u o", u=1))
         w_sb = keep.tile([P, 2048], BF16, name="w_sb")
         nc.sync.dma_start(out=w_sb[:, 0:1024], in_=weight.rearrange("o c i j -> o (c i j)"))
@@ -71,7 +70,7 @@ def tile_customconvmodule_t_kernel(tc, x, weight, bias, out):
         tws = {}
 
         def turn_w(i, j):
-            tw = psw.tile([P, 512], F32, name="tw")
+            tw = psum.tile([P, 512], F32, name="bank")
             view = tw[:].rearrange("q (o t) -> q o t", t=4)
             for t in range(4):
                 first = 4 * t + 2 * i + j
@@ -142,7 +141,7 @@ def tile_customconvmodule_t_kernel(tc, x, weight, bias, out):
             width = 64 * (hi - lo)
             for j, g in order:
                 if j == 1:
-                    acc = psa.tile([P, 512], F32, name="acc")
+                    acc = psum.tile([P, 512], F32, name="bank")
                     accs[(u, g)] = acc
                 acc = accs[(u, g)]
                 for i in range(2):
@@ -215,6 +214,9 @@ def tile_customconvmodule_t_kernel(tc, x, weight, bias, out):
         gather_w(vec, 1, 1)
         gather_w(act, 0, 0)
         gather_w(act, 1, 0)
+        b_col = psum.tile([P, 512], F32, name="bank")
+        nc.tensor.matmul(b_col[:, 0:1], lhsT=b_row[:], rhs=ident[:, 0:1], start=True, stop=True)
+        act(out=b32[:], in_=b_col[:, 0:1])
         quantise_w(1)
         quantise(0)
         stuff_w(1)
@@ -227,13 +229,9 @@ def tile_customconvmodule_t_kernel(tc, x, weight, bias, out):
         regroup_unit(2)
         shift_codes(1)
         shift_planes(1)
-        by_dma = (3, 4, 5, 6)
+        by_dma = ()
         for u in range(LAST + 1):
             passes(u, both if u < LAST else in_turn)
-            if u == 0:
-                b_col = psw.tile([P, 512], F32, name="tw")
-                nc.tensor.matmul(b_col[:, 0:1], lhsT=b_row[:], rhs=ident[:, 0:1], start=True, stop=True)
-                act(out=b32[:], in_=b_col[:, 0:1])
             if u + 2 <= LAST:
                 quantise(u + 2)
                 if u + 2 in by_dma:

@@ -28,23 +28,47 @@ def tile_customconvmodule_t_kernel(tc, x, weight, bias, out):
         keep = ctx.enter_context(tc.tile_pool(name="keep", bufs=1))
         psum = ctx.enter_context(tc.psum_pool(name="psum", bufs=8))
         ctx.enter_context(tc.manual_schedule())
+        vec = nc.vector.tensor_copy
+        act = nc.scalar.copy
+        lower = slice(0, 64)
+        upper = slice(64, 128)
 
         b_row = keep.tile([P, P], BF16, name="b_row")
         nc.gpsimd.memset(b_row[:].bitcast(I32), 0)
         nc.scalar.dma_start(out=b_row[0:1, :], in_=bias.rearrange("(u o) -> u o", u=1))
-        w_sb = keep.tile([P, 2048], BF16, name="w_sb")
+        table = keep.tile([P, 2], BF16, name="table")
+        nc.gpsimd.memset(table[:], 0)
+        w_sb = keep.tile([P, 2050], BF16, name="w_sb")
         nc.sync.dma_start(out=w_sb[:, 0:1024], in_=weight.rearrange("o c i j -> o (c i j)"))
+        nc.scalar.copy(out=table[:, 0:1], in_=table[:, 1:2])
         xv = x.rearrange("b c h w -> (b c h w)").rearrange("(n q f) -> n q f", n=PAIRS, q=P)
-        raw = []
-        for n in range(PAIRS):
-            r = keep.tile([P, 3844], BF16, name="raw%d" % n)
-            raw.append(r)
-            nc.sync.dma_start(out=r[:], in_=xv[n])
+        parts = {}
+        for s, k, first, rows in ((0, 0, 1, 8), (1, 0, 0, 9), (0, 1, 9, 8), (1, 1, 9, 7)):
+            part = keep.tile([P, 4, 280], BF16, name="raw0%d%d" % (s, k))
+            h = 16 * s + first - 1
+            nc.sync.dma_start(
+                out=part[:, :, 0 : 31 * rows],
+                in_=xv[0].rearrange("q (t f) -> q t f", t=4)[:, :, 31 * h : 31 * (h + rows)],
+            )
+            parts[(0, s, k)] = (part[:, :, 0 : 31 * rows].rearrange("q t (h w) -> q t h w", w=31), first)
+
+        def load(n):
+            raw = keep.tile([P, 3844], BF16, name="raw%d" % n)
+            nc.sync.dma_start(out=raw[:], in_=xv[n])
+            view = raw[:].rearrange("q (t h w) -> q t h w", t=4, w=31)
+            for k in range(2):
+                parts[(n, 0, k)] = (view, 1)
+                parts[(n, 1, k)] = (view[:, :, 15:31, :], 0)
+
+        load(1)
 
         ident = keep.tile([P, P], BF16, name="ident")
         make_identity(nc, ident[:])
         w_a = keep.tile([P, 512], U32, name="w_a", align_bytes=64)
         w_b = keep.tile([P, 512], U32, name="w_b", align_bytes=64)
+        w_q = keep.tile([P, 256], U32, name="w_q", align_bytes=64)
+        w_s = keep.tile([P, 256], U8, name="w_s", align_bytes=64)
+        w_x = keep.tile([P, 256], U8, name="w_x", align_bytes=64)
         grp_all = keep.tile([P, PAIRS, COLS * 4], BF16, name="grp", align_bytes=64)
         codes_all = keep.tile([P, PAIRS, 16 + COLS], U32, name="codes", align_bytes=64)
         planes_all = keep.tile([P, PAIRS, 64 + COLS], U8, name="planes", align_bytes=64)
@@ -57,79 +81,88 @@ def tile_customconvmodule_t_kernel(tc, x, weight, bias, out):
         planes_r = [planes_r_all[:, n, :] for n in range(PAIRS)]
         gm = grp_all[:].bitcast(I32).rearrange("q n (m e) -> q n m e", e=64)
         nc.vector.memset(gm[:, :, :, 56:64], 0)
-        nc.vector.memset(w_a[64:128, :].bitcast(I32), 0)
-        nc.vector.memset(w_b[0:64, :].bitcast(I32), 0)
+        nc.vector.memset(w_a[upper, :].bitcast(I32), 0)
+        nc.vector.memset(w_b[lower, :].bitcast(I32), 0)
+
         b32 = keep.tile([P, 1], F32, name="b32")
 
         def regroup(copy, n, s, lo, hi):
-            src = raw[n][:].rearrange("q (t h w) -> q t h w", t=4, h=31)
-            src = src[:, :, 16 * s + lo - 1 : 16 * s + hi - 1, :].rearrange("q t h w -> q h w t")
+            part, first = parts[(n, s, 0 if lo < 9 else 1)]
+            src = part[:, :, lo - first : hi - first, :].rearrange("q t h w -> q h w t")
             dst = grp[n].rearrange("q (r s w t) -> q r s w t", r=ROWS, s=2, w=32)
             copy(out=dst[:, lo:hi, s, 0:31, :], in_=src)
 
         tws = {}
 
-        def turn_w(i, j):
+        def turn_w(j):
             tw = psum.tile([P, 512], F32, name="bank")
             view = tw[:].rearrange("q (o t) -> q o t", t=4)
             for t in range(4):
-                first = 4 * t + 2 * i + j
-                nc.tensor.matmul(view[:, :, t], lhsT=w_sb[:, first : 2048 : 16], rhs=ident[:], start=True, stop=True)
-            tws[(i, j)] = tw
+                first = 4 * t + 2 + j
+                nc.tensor.matmul(
+                    view[:, :, t], lhsT=w_sb[:, first : first + 2033 : 16], rhs=ident[:], start=True, stop=True
+                )
+            tws[j] = tw
 
-        gw = keep.tile([P, 2048], BF16, name="gw", align_bytes=64)
+        gw = keep.tile([P, 1024], BF16, name="gw", align_bytes=64)
 
-        def gather_w(copy, i, j):
-            c0 = 1024 * j + 512 * i
-            copy(out=gw[:, c0 : c0 + 512], in_=tws[(i, j)][:])
-
-        w_q = keep.tile([P, 512], U32, name="w_q", align_bytes=64)
-        w_s = keep.tile([P, 512], U8, name="w_s", align_bytes=64)
-        w_half = [w_a, w_b]
+        def gather_w(copy, j):
+            copy(out=gw[:, 512 * j : 512 * j + 512], in_=tws[j][:])
 
         def quantise_w(j):
             nc.vector.quantize_mx(
-                out=w_q[:, 256 * j : 256 * j + 256].bitcast(FP8X4),
-                scales=w_s[:, 256 * j : 256 * j + 256],
-                in_=gw[:, 1024 * j : 1024 * j + 1024],
+                out=w_q[:, 128 * j : 128 * j + 128].bitcast(FP8X4),
+                scales=w_s[:, 128 * j : 128 * j + 128],
+                in_=gw[:, 512 * j : 512 * j + 512],
             )
 
-        def stuff_w(j):
-            for half, lo in ((w_a, 0), (w_b, 64)):
-                nc.vector.tensor_copy(
-                    out=half[lo : lo + 64, 256 * j : 256 * j + 256].bitcast(I32),
-                    in_=w_q[lo : lo + 64, 256 * j : 256 * j + 256].bitcast(I32),
-                )
+        def cross_w(j0, j1):
+            c0, c1 = 128 * j0, 128 * j1
+            nc.sync.dma_start(out=w_a[lower, c0:c1].bitcast(I32), in_=w_q[upper, c0:c1].bitcast(I32))
+            nc.sync.dma_start(out=w_x[lower, c0:c1].bitcast(I32), in_=w_s[upper, c0:c1].bitcast(I32))
+            nc.sync.dma_start(out=w_b[upper, 256 + c0 : 256 + c1].bitcast(I32), in_=w_q[lower, c0:c1].bitcast(I32))
+            nc.sync.dma_start(out=w_x[upper, c0:c1].bitcast(I32), in_=w_s[lower, c0:c1].bitcast(I32))
 
-        vec = nc.vector.tensor_copy
-        act = nc.scalar.copy
+        def stuff_w(j):
+            c0, c1 = 128 * j, 128 * j + 128
+            vec(out=w_a[lower, 256 + c0 : 256 + c1].bitcast(I32), in_=w_q[lower, c0:c1].bitcast(I32))
+            vec(out=w_b[upper, c0:c1].bitcast(I32), in_=w_q[upper, c0:c1].bitcast(I32))
+
+        def keep_warm(count):
+            spare = psum.tile([P, 512], F32, name="bank")
+            for d in range(count):
+                nc.tensor.matmul(spare[:], lhsT=ident[:], rhs=w_sb[:, 0:512], start=True, stop=True)
+
+        def bias_column():
+            b_col = psum.tile([P, 512], F32, name="bank")
+            nc.tensor.matmul(b_col[:, 0:1], lhsT=b_row[:], rhs=ident[:, 0:1], start=True, stop=True)
+            act(out=b32[:], in_=b_col[:, 0:1])
 
         def columns(u):
             n, lo, hi = UNITS[u]
             return (0 if lo == 0 else 64 * (lo + 1)), 64 * (hi + 1)
 
-        def quantise(u, part=None):
+        def quantise(u):
             n = UNITS[u][0]
             c0, c1 = columns(u)
-            pieces = [(c0, c1)] if c0 else [(0, c1 - 64), (c1 - 64, c1)]
-            for a, b in pieces if part is None else [pieces[part]]:
+            for a, b in [(c0, c1)] if c0 else [(0, c1 - 64), (c1 - 64, c1)]:
                 nc.vector.quantize_mx(
                     out=codes[n][:, 16 + a : 16 + b].bitcast(FP8X4),
                     scales=planes[n][:, 64 + a : 64 + b],
                     in_=grp[n][:, 4 * a : 4 * b],
                 )
 
-        def shift_codes(u, queue=None):
+        def shift_codes(u, move=nc.vector.tensor_copy):
             n = UNITS[u][0]
             c0, c1 = columns(u)
-            move = nc.vector.tensor_copy if queue is None else queue.dma_start
             move(out=codes_r[n][:, c0:c1].bitcast(I32), in_=codes[n][:, 15 + c0 : 15 + c1].bitcast(I32))
 
         def shift_planes(u):
             n = UNITS[u][0]
             c0, c1 = columns(u)
-            nc.vector.tensor_copy(out=planes_r[n][:, c0:c1], in_=planes[n][:, 63 + c0 : 63 + c1])
+            vec(out=planes_r[n][:, c0:c1], in_=planes[n][:, 63 + c0 : 63 + c1])
 
+        w_half = [w_a, w_b]
         res = {}
         for n in range(PAIRS):
             for g in range(2):
@@ -139,29 +172,28 @@ def tile_customconvmodule_t_kernel(tc, x, weight, bias, out):
         def passes(u, order):
             n, lo, hi = UNITS[u]
             width = 64 * (hi - lo)
-            for j, g in order:
+            done = [0, 0]
+            for g, j, i in order:
+                if done[g] == 0:
+                    accs[(u, g)] = psum.tile([P, 512], F32, name="bank")
+                done[g] += 1
+                tap = 2 * i + j
+                c0 = (lo + i) * 64
                 if j == 1:
-                    acc = psum.tile([P, 512], F32, name="bank")
-                    accs[(u, g)] = acc
-                acc = accs[(u, g)]
-                for i in range(2):
-                    tap = 2 * j + i
-                    c0 = (lo + i) * 64
-                    if j == 1:
-                        x_codes = codes[n][:, 16 + c0 : 16 + c0 + width]
-                        x_plane = planes[n][:, 64 + c0 : 64 + c0 + width]
-                    else:
-                        x_codes = codes_r[n][:, c0 : c0 + width]
-                        x_plane = planes_r[n][:, c0 : c0 + width]
-                    nc.tensor.matmul_mx(
-                        out=acc[:, 0:width],
-                        lhsT=w_half[g][:, tap * P : (tap + 1) * P].bitcast(FP8X4),
-                        lhsT_scale=w_s[:, tap * P : (tap + 1) * P],
-                        rhs=x_codes.bitcast(FP8X4),
-                        rhs_scale=x_plane,
-                        start=(j == 1 and i == 0),
-                        stop=(j == 0 and i == 1),
-                    )
+                    x_codes = codes[n][:, 16 + c0 : 16 + c0 + width]
+                    x_plane = planes[n][:, 64 + c0 : 64 + c0 + width]
+                else:
+                    x_codes = codes_r[n][:, c0 : c0 + width]
+                    x_plane = planes_r[n][:, c0 : c0 + width]
+                nc.tensor.matmul_mx(
+                    out=accs[(u, g)][:, 0:width],
+                    lhsT=w_half[g][:, tap * P : (tap + 1) * P].bitcast(FP8X4),
+                    lhsT_scale=(w_s if i != g else w_x)[:, j * P : (j + 1) * P],
+                    rhs=x_codes.bitcast(FP8X4),
+                    rhs_scale=x_plane,
+                    start=(done[g] == 1),
+                    stop=(done[g] == 4),
+                )
 
         def evacuate(u, g, on_vector=False):
             n, lo, hi = UNITS[u]
@@ -181,9 +213,10 @@ def tile_customconvmodule_t_kernel(tc, x, weight, bias, out):
             elif hi == 16:
                 nc.sync.dma_start(out=out[2 * n + g].rearrange("o y z -> o (y z)"), in_=res[(n, g)][:])
 
-        both = ((1, 0), (1, 1), (0, 0), (0, 1))
-        in_turn = ((1, 0), (0, 0), (1, 1), (0, 1))
-
+        corners = ((0, 0), (0, 1), (1, 0), (1, 1))
+        own_first = [(g, j, i) for own in (True, False) for j in (1, 0) for g, i in corners if (g != i) == own]
+        both = [(g, j, i) for j in (1, 0) for g in (0, 1) for i in (0, 1)]
+        in_turn = [(g, j, i) for g in (0, 1) for j in (1, 0) for i in (0, 1)]
         shares = (
             ((act, 1, 2, 9), (vec, 0, 1, 9), (vec, 1, 0, 2)),
             ((act, 1, 9, 16), (act, 0, 13, 17), (vec, 0, 9, 13)),
@@ -200,28 +233,28 @@ def tile_customconvmodule_t_kernel(tc, x, weight, bias, out):
             for copy, s, lo, hi in shares[u]:
                 regroup(copy, UNITS[u][0], s, lo, hi)
 
-        vec(out=w_sb[:, 1024:2048], in_=w_sb[:, 0:1024])
+        vec(out=w_sb[:, 1026:2050], in_=w_sb[:, 0:1024])
+        nc.vector.memset(w_s[:].bitcast(I32), 0)
         nc.vector.memset(gm[:, :, 0, 0:56], 0)
         nc.vector.memset(gm[:, :, 2 * ROWS - 1, 0:56], 0)
         nc.vector.memset(codes_all[:, :, 0:16].bitcast(I32), 0)
         nc.vector.memset(planes_all[:].bitcast(I32), 0)
-        turn_w(0, 1)
-        turn_w(1, 1)
-        turn_w(0, 0)
-        turn_w(1, 0)
-        gather_w(act, 0, 1)
+        turn_w(1)
+        turn_w(0)
         regroup_unit(0)
-        gather_w(vec, 1, 1)
-        gather_w(act, 0, 0)
-        gather_w(act, 1, 0)
-        b_col = psum.tile([P, 512], F32, name="bank")
-        nc.tensor.matmul(b_col[:, 0:1], lhsT=b_row[:], rhs=ident[:, 0:1], start=True, stop=True)
-        act(out=b32[:], in_=b_col[:, 0:1])
-        quantise_w(1)
+        keep_warm(5)
+        gather_w(act, 1)
+        gather_w(act, 0)
+        bias_column()
         quantise(0)
+        quantise_w(1)
+        cross_w(1, 2)
+        shift_codes(0)
         stuff_w(1)
         quantise_w(0)
-        shift_codes(0)
+        cross_w(0, 1)
+        load(2)
+        load(3)
         shift_planes(0)
         stuff_w(0)
         regroup_unit(1)
@@ -231,11 +264,11 @@ def tile_customconvmodule_t_kernel(tc, x, weight, bias, out):
         shift_planes(1)
         by_dma = ()
         for u in range(LAST + 1):
-            passes(u, both if u < LAST else in_turn)
+            passes(u, own_first if u == 0 else both if u < LAST else in_turn)
             if u + 2 <= LAST:
                 quantise(u + 2)
                 if u + 2 in by_dma:
-                    shift_codes(u + 2, nc.sync)
+                    shift_codes(u + 2, nc.sync.dma_start)
             if u + 3 <= LAST:
                 regroup_unit(u + 3)
             if u + 2 <= LAST:

@@ -18,7 +18,7 @@ P = 128
 PAIRS = 4
 ROWS = 17
 COLS = ROWS * 64
-UNITS = ((0, 0, 8), (0, 8, 16), (1, 0, 8), (1, 8, 16), (2, 0, 8), (2, 8, 16), (3, 0, 8), (3, 8, 12), (3, 12, 16))
+UNITS = ((0, 0, 8), (0, 8, 16), (1, 0, 8), (1, 8, 16), (2, 0, 8), (2, 8, 16), (3, 0, 8), (3, 8, 12), (3, 12, 14), (3, 14, 16))
 LAST = len(UNITS) - 1
 
 
@@ -81,8 +81,9 @@ def tile_customconvmodule_t_kernel(tc, x, weight, bias, out):
         planes_r = [planes_r_all[:, n, :] for n in range(PAIRS)]
         gm = grp_all[:].bitcast(I32).rearrange("q n (m e) -> q n m e", e=64)
         nc.vector.memset(gm[:, :, :, 56:64], 0)
-        nc.vector.memset(w_a[upper, :].bitcast(I32), 0)
-        nc.vector.memset(w_b[lower, :].bitcast(I32), 0)
+        nc.gpsimd.memset(w_a[upper, :].bitcast(I32), 0)
+        nc.gpsimd.memset(w_b[lower, :].bitcast(I32), 0)
+        nc.vector.memset(planes_all[:].bitcast(I32), 0)
 
         b32 = keep.tile([P, 1], F32, name="b32")
 
@@ -133,10 +134,10 @@ def tile_customconvmodule_t_kernel(tc, x, weight, bias, out):
             for d in range(count):
                 nc.tensor.matmul(spare[:], lhsT=ident[:], rhs=w_sb[:, 0:512], start=True, stop=True)
 
-        def bias_column():
+        def bias_matmul():
             b_col = psum.tile([P, 512], F32, name="bank")
             nc.tensor.matmul(b_col[:, 0:1], lhsT=b_row[:], rhs=ident[:, 0:1], start=True, stop=True)
-            act(out=b32[:], in_=b_col[:, 0:1])
+            return b_col
 
         def columns(u):
             n, lo, hi = UNITS[u]
@@ -218,7 +219,7 @@ def tile_customconvmodule_t_kernel(tc, x, weight, bias, out):
         both = [(g, j, i) for j in (1, 0) for g in (0, 1) for i in (0, 1)]
         in_turn = [(g, j, i) for g in (0, 1) for j in (1, 0) for i in (0, 1)]
         shares = (
-            ((act, 1, 2, 9), (vec, 0, 1, 9), (vec, 1, 0, 2)),
+            ((act, 1, 4, 9), (vec, 0, 1, 9), (vec, 1, 0, 4)),
             ((act, 1, 9, 16), (act, 0, 13, 17), (vec, 0, 9, 13)),
             ((act, 1, 2, 9), (vec, 0, 1, 9), (vec, 1, 0, 2)),
             ((act, 1, 11, 16), (vec, 0, 9, 17), (vec, 1, 9, 11)),
@@ -226,7 +227,8 @@ def tile_customconvmodule_t_kernel(tc, x, weight, bias, out):
             ((act, 1, 11, 16), (vec, 0, 9, 17), (vec, 1, 9, 11)),
             ((act, 1, 2, 9), (vec, 0, 1, 9), (vec, 1, 0, 2)),
             ((act, 1, 11, 13), (vec, 0, 9, 13), (vec, 1, 9, 11)),
-            ((act, 1, 13, 16), (vec, 0, 13, 17)),
+            ((act, 1, 13, 15), (vec, 0, 13, 15)),
+            ((act, 1, 15, 16), (vec, 0, 15, 17)),
         )
 
         def regroup_unit(u):
@@ -238,14 +240,14 @@ def tile_customconvmodule_t_kernel(tc, x, weight, bias, out):
         nc.vector.memset(gm[:, :, 0, 0:56], 0)
         nc.vector.memset(gm[:, :, 2 * ROWS - 1, 0:56], 0)
         nc.vector.memset(codes_all[:, :, 0:16].bitcast(I32), 0)
-        nc.vector.memset(planes_all[:].bitcast(I32), 0)
         turn_w(1)
         turn_w(0)
+        b_col = bias_matmul()
+        keep_warm(4)
         regroup_unit(0)
-        keep_warm(5)
         gather_w(act, 1)
         gather_w(act, 0)
-        bias_column()
+        act(out=b32[:], in_=b_col[:, 0:1])
         quantise(0)
         quantise_w(1)
         cross_w(1, 2)

@@ -64,11 +64,9 @@ def tile_customconvmodule_t_kernel(tc, x, weight, bias, out):
 
         ident = keep.tile([P, P], BF16, name="ident")
         make_identity(nc, ident[:])
-        w_a = keep.tile([P, 512], U32, name="w_a", align_bytes=64)
-        w_b = keep.tile([P, 512], U32, name="w_b", align_bytes=64)
-        w_q = keep.tile([P, 256], U32, name="w_q", align_bytes=64)
-        w_s = keep.tile([P, 256], U8, name="w_s", align_bytes=64)
-        w_x = keep.tile([P, 256], U8, name="w_x", align_bytes=64)
+        w_q = keep.tile([P, 320], U32, name="w_q", align_bytes=64)
+        w_own = [keep.tile([P, 256], U32, name="w_own%d" % g, align_bytes=64) for g in range(2)]
+        w_other = [keep.tile([P, 320], U32, name="w_other%d" % g, align_bytes=64) for g in range(2)]
         grp_all = keep.tile([P, PAIRS, COLS * 4], BF16, name="grp", align_bytes=64)
         codes_all = keep.tile([P, PAIRS, 16 + COLS], U32, name="codes", align_bytes=64)
         planes_all = keep.tile([P, PAIRS, 64 + COLS], U8, name="planes", align_bytes=64)
@@ -81,9 +79,11 @@ def tile_customconvmodule_t_kernel(tc, x, weight, bias, out):
         planes_r = [planes_r_all[:, n, :] for n in range(PAIRS)]
         gm = grp_all[:].bitcast(I32).rearrange("q n (m e) -> q n m e", e=64)
         nc.vector.memset(gm[:, :, :, 56:64], 0)
-        nc.gpsimd.memset(w_a[upper, :].bitcast(I32), 0)
-        nc.gpsimd.memset(w_b[lower, :].bitcast(I32), 0)
+        for g, half in ((0, upper), (1, lower)):
+            nc.gpsimd.memset(w_own[g][half, :].bitcast(I32), 0)
+            nc.gpsimd.memset(w_other[g][half, :].bitcast(I32), 0)
         nc.vector.memset(planes_all[:].bitcast(I32), 0)
+        nc.gpsimd.memset(w_q[:].rearrange("q (j w) -> q j w", j=2)[:, :, 128:160].bitcast(I32), 0)
 
         b32 = keep.tile([P, 1], F32, name="b32")
 
@@ -110,24 +110,28 @@ def tile_customconvmodule_t_kernel(tc, x, weight, bias, out):
         def gather_w(copy, j):
             copy(out=gw[:, 512 * j : 512 * j + 512], in_=tws[j][:])
 
+        def w_codes(tile, j):
+            return tile[:, 160 * j : 160 * j + 128]
+
+        def w_scales(tile, j):
+            return tile[:].bitcast(U8)[:, 640 * j + 512 : 640 * j + 640]
+
         def quantise_w(j):
             nc.vector.quantize_mx(
-                out=w_q[:, 128 * j : 128 * j + 128].bitcast(FP8X4),
-                scales=w_s[:, 128 * j : 128 * j + 128],
-                in_=gw[:, 512 * j : 512 * j + 512],
+                out=w_codes(w_q, j).bitcast(FP8X4), scales=w_scales(w_q, j), in_=gw[:, 512 * j : 512 * j + 512]
             )
 
         def cross_w(j0, j1):
-            c0, c1 = 128 * j0, 128 * j1
-            nc.sync.dma_start(out=w_a[lower, c0:c1].bitcast(I32), in_=w_q[upper, c0:c1].bitcast(I32))
-            nc.sync.dma_start(out=w_x[lower, c0:c1].bitcast(I32), in_=w_s[upper, c0:c1].bitcast(I32))
-            nc.sync.dma_start(out=w_b[upper, 256 + c0 : 256 + c1].bitcast(I32), in_=w_q[lower, c0:c1].bitcast(I32))
-            nc.sync.dma_start(out=w_x[upper, c0:c1].bitcast(I32), in_=w_s[lower, c0:c1].bitcast(I32))
+            c0, c1 = 160 * j0, 160 * j1
+            nc.sync.dma_start(out=w_other[0][lower, c0:c1].bitcast(I32), in_=w_q[upper, c0:c1].bitcast(I32))
+            nc.sync.dma_start(out=w_other[1][upper, c0:c1].bitcast(I32), in_=w_q[lower, c0:c1].bitcast(I32))
 
         def stuff_w(j):
-            c0, c1 = 128 * j, 128 * j + 128
-            vec(out=w_a[lower, 256 + c0 : 256 + c1].bitcast(I32), in_=w_q[lower, c0:c1].bitcast(I32))
-            vec(out=w_b[upper, c0:c1].bitcast(I32), in_=w_q[upper, c0:c1].bitcast(I32))
+            for g, half in ((0, lower), (1, upper)):
+                vec(
+                    out=w_own[g][half, 128 * j : 128 * j + 128].bitcast(I32),
+                    in_=w_q[half, 160 * j : 160 * j + 128].bitcast(I32),
+                )
 
         def keep_warm(count):
             spare = psum.tile([P, 512], F32, name="bank")
@@ -163,7 +167,6 @@ def tile_customconvmodule_t_kernel(tc, x, weight, bias, out):
             c0, c1 = columns(u)
             vec(out=planes_r[n][:, c0:c1], in_=planes[n][:, 63 + c0 : 63 + c1])
 
-        w_half = [w_a, w_b]
         res = {}
         for n in range(PAIRS):
             for g in range(2):
@@ -178,7 +181,12 @@ def tile_customconvmodule_t_kernel(tc, x, weight, bias, out):
                 if done[g] == 0:
                     accs[(u, g)] = psum.tile([P, 512], F32, name="bank")
                 done[g] += 1
-                tap = 2 * i + j
+                if i != g:
+                    w_part = w_own[g][:, 128 * j : 128 * j + 128]
+                    w_plane = w_scales(w_q, j)
+                else:
+                    w_part = w_codes(w_other[g], j)
+                    w_plane = w_scales(w_other[g], j)
                 c0 = (lo + i) * 64
                 if j == 1:
                     x_codes = codes[n][:, 16 + c0 : 16 + c0 + width]
@@ -188,8 +196,8 @@ def tile_customconvmodule_t_kernel(tc, x, weight, bias, out):
                     x_plane = planes_r[n][:, c0 : c0 + width]
                 nc.tensor.matmul_mx(
                     out=accs[(u, g)][:, 0:width],
-                    lhsT=w_half[g][:, tap * P : (tap + 1) * P].bitcast(FP8X4),
-                    lhsT_scale=(w_s if i != g else w_x)[:, j * P : (j + 1) * P],
+                    lhsT=w_part.bitcast(FP8X4),
+                    lhsT_scale=w_plane,
                     rhs=x_codes.bitcast(FP8X4),
                     rhs_scale=x_plane,
                     start=(done[g] == 1),
@@ -219,7 +227,7 @@ def tile_customconvmodule_t_kernel(tc, x, weight, bias, out):
         both = [(g, j, i) for j in (1, 0) for g in (0, 1) for i in (0, 1)]
         in_turn = [(g, j, i) for g in (0, 1) for j in (1, 0) for i in (0, 1)]
         shares = (
-            ((act, 1, 4, 9), (vec, 0, 1, 9), (vec, 1, 0, 4)),
+            ((act, 1, 2, 9), (vec, 0, 1, 9), (vec, 1, 0, 2)),
             ((act, 1, 9, 16), (act, 0, 13, 17), (vec, 0, 9, 13)),
             ((act, 1, 2, 9), (vec, 0, 1, 9), (vec, 1, 0, 2)),
             ((act, 1, 11, 16), (vec, 0, 9, 17), (vec, 1, 9, 11)),
@@ -236,7 +244,6 @@ def tile_customconvmodule_t_kernel(tc, x, weight, bias, out):
                 regroup(copy, UNITS[u][0], s, lo, hi)
 
         vec(out=w_sb[:, 1026:2050], in_=w_sb[:, 0:1024])
-        nc.vector.memset(w_s[:].bitcast(I32), 0)
         nc.vector.memset(gm[:, :, 0, 0:56], 0)
         nc.vector.memset(gm[:, :, 2 * ROWS - 1, 0:56], 0)
         nc.vector.memset(codes_all[:, :, 0:16].bitcast(I32), 0)
@@ -245,18 +252,18 @@ def tile_customconvmodule_t_kernel(tc, x, weight, bias, out):
         b_col = bias_matmul()
         keep_warm(4)
         regroup_unit(0)
-        gather_w(act, 1)
+        gather_w(vec, 1)
         gather_w(act, 0)
         act(out=b32[:], in_=b_col[:, 0:1])
-        quantise(0)
         quantise_w(1)
         cross_w(1, 2)
-        shift_codes(0)
-        stuff_w(1)
+        quantise(0)
         quantise_w(0)
         cross_w(0, 1)
         load(2)
         load(3)
+        stuff_w(1)
+        shift_codes(0)
         shift_planes(0)
         stuff_w(0)
         regroup_unit(1)

@@ -227,10 +227,10 @@ def tile_customconvmodule_t_kernel(tc, x, weight, bias, out):
         both = [(g, j, i) for j in (1, 0) for g in (0, 1) for i in (0, 1)]
         in_turn = [(g, j, i) for g in (0, 1) for j in (1, 0) for i in (0, 1)]
         shares = (
-            ((act, 1, 2, 9), (vec, 0, 1, 9), (vec, 1, 0, 2)),
-            ((act, 1, 9, 16), (act, 0, 13, 17), (vec, 0, 9, 13)),
-            ((act, 1, 2, 9), (vec, 0, 1, 9), (vec, 1, 0, 2)),
-            ((act, 1, 11, 16), (vec, 0, 9, 17), (vec, 1, 9, 11)),
+            ((act, 1, 4, 9), (vec, 0, 1, 9), (vec, 1, 0, 4)),
+            ((act, 1, 9, 16), (act, 0, 11, 17), (vec, 0, 9, 11)),
+            ((act, 1, 0, 9), (vec, 0, 1, 9)),
+            ((act, 1, 9, 16), (vec, 0, 9, 17)),
             ((act, 1, 2, 9), (vec, 0, 1, 9), (vec, 1, 0, 2)),
             ((act, 1, 11, 16), (vec, 0, 9, 17), (vec, 1, 9, 11)),
             ((act, 1, 2, 9), (vec, 0, 1, 9), (vec, 1, 0, 2)),
@@ -250,14 +250,14 @@ def tile_customconvmodule_t_kernel(tc, x, weight, bias, out):
         turn_w(1)
         turn_w(0)
         b_col = bias_matmul()
-        keep_warm(4)
+        keep_warm(2)
         regroup_unit(0)
-        gather_w(vec, 1)
+        gather_w(act, 1)
         gather_w(act, 0)
         act(out=b32[:], in_=b_col[:, 0:1])
+        quantise(0)
         quantise_w(1)
         cross_w(1, 2)
-        quantise(0)
         quantise_w(0)
         cross_w(0, 1)
         load(2)

from contextlib import ExitStack

import concourse.mybir as mybir
from concourse.masks import make_identity

BF16 = mybir.dt.bfloat16
F32 = mybir.dt.float32
I32 = mybir.dt.int32
U32 = mybir.dt.uint32
U8 = mybir.dt.uint8
FP8X4 = mybir.dt.float8_e4m3fn_x4
IDENT = mybir.ActivationFunctionType.Identity
ADD = mybir.AluOpType.add

FLOPS = 2 * 8192 * 1024 * 128

P = 128
PAIRS = 4
ROWS = 17
COLS = ROWS * 64
UNITS = ((0, 0, 8), (0, 8, 16), (1, 0, 8), (1, 8, 16), (2, 0, 8), (2, 8, 16), (3, 0, 8), (3, 8, 12), (3, 12, 14), (3, 14, 16))
LAST = len(UNITS) - 1


def tile_customconvmodule_t_kernel(tc, x, weight, bias, out):
    nc = tc.nc
    with ExitStack() as ctx:
        keep = ctx.enter_context(tc.tile_pool(name="keep", bufs=1))
        psum = ctx.enter_context(tc.psum_pool(name="psum", bufs=8))
        ctx.enter_context(tc.manual_schedule())
        vec = nc.vector.tensor_copy
        act = nc.scalar.copy
        lower = slice(0, 64)
        upper = slice(64, 128)

        b_row = keep.tile([P, P], BF16, name="b_row")
        nc.gpsimd.memset(b_row[:].bitcast(I32), 0)
        nc.scalar.dma_start(out=b_row[0:1, :], in_=bias.rearrange("(u o) -> u o", u=1))
        table = keep.tile([P, 2], BF16, name="table")
        nc.gpsimd.memset(table[:], 0)
        w_sb = keep.tile([P, 2050], BF16, name="w_sb")
        nc.sync.dma_start(out=w_sb[:, 0:1024], in_=weight.rearrange("o c i j -> o (c i j)"))
        nc.scalar.copy(out=table[:, 0:1], in_=table[:, 1:2])
        xv = x.rearrange("b c h w -> (b c h w)").rearrange("(n q f) -> n q f", n=PAIRS, q=P)
        parts = {}
        for s, k, first, rows in ((0, 0, 1, 8), (1, 0, 0, 9), (0, 1, 9, 8), (1, 1, 9, 7)):
            part = keep.tile([P, 4, 280], BF16, name="raw0%d%d" % (s, k))
            h = 16 * s + first - 1
            nc.sync.dma_start(
                out=part[:, :, 0 : 31 * rows],
                in_=xv[0].rearrange("q (t f) -> q t f", t=4)[:, :, 31 * h : 31 * (h + rows)],
            )
            parts[(0, s, k)] = (part[:, :, 0 : 31 * rows].rearrange("q t (h w) -> q t h w", w=31), first)

        def load(n):
            raw = keep.tile([P, 3844], BF16, name="raw%d" % n)
            nc.sync.dma_start(out=raw[:], in_=xv[n])
            view = raw[:].rearrange("q (t h w) -> q t h w", t=4, w=31)
            for k in range(2):
                parts[(n, 0, k)] = (view, 1)
                parts[(n, 1, k)] = (view[:, :, 15:31, :], 0)

        load(1)

        ident = keep.tile([P, P], BF16, name="ident")
        make_identity(nc, ident[:])
        w_q = keep.tile([P, 320], U32, name="w_q", align_bytes=64)
        w_own = [keep.tile([P, 256], U32, name="w_own%d" % g, align_bytes=64) for g in range(2)]
        w_other = [keep.tile([P, 320], U32, name="w_other%d" % g, align_bytes=64) for g in range(2)]
        grp_all = keep.tile([P, PAIRS, COLS * 4], BF16, name="grp", align_bytes=64)
        codes_all = keep.tile([P, PAIRS, 16 + COLS], U32, name="codes", align_bytes=64)
        planes_all = keep.tile([P, PAIRS, 64 + COLS], U8, name="planes", align_bytes=64)
        codes_r_all = keep.tile([P, PAIRS, COLS], U32, name="codes_r", align_bytes=64)
        planes_r_all = keep.tile([P, PAIRS, COLS], U8, name="planes_r", align_bytes=64)
        grp = [grp_all[:, n, :] for n in range(PAIRS)]
        codes = [codes_all[:, n, :] for n in range(PAIRS)]
        planes = [planes_all[:, n, :] for n in range(PAIRS)]
        codes_r = [codes_r_all[:, n, :] for n in range(PAIRS)]
        planes_r = [planes_r_all[:, n, :] for n in range(PAIRS)]
        gm = grp_all[:].bitcast(I32).rearrange("q n (m e) -> q n m e", e=64)
        nc.vector.memset(gm[:, :, :, 56:64], 0)
        for g, half in ((0, upper), (1, lower)):
            nc.gpsimd.memset(w_own[g][half, :].bitcast(I32), 0)
            nc.gpsimd.memset(w_other[g][half, :].bitcast(I32), 0)
        nc.vector.memset(planes_all[:].bitcast(I32), 0)
        nc.gpsimd.memset(w_q[:].rearrange("q (j w) -> q j w", j=2)[:, :, 128:160].bitcast(I32), 0)

        b32 = keep.tile([P, 1], F32, name="b32")

        def regroup(copy, n, s, lo, hi):
            part, first = parts[(n, s, 0 if lo < 9 else 1)]
            src = part[:, :, lo - first : hi - first, :].rearrange("q t h w -> q h w t")
            dst = grp[n].rearrange("q (r s w t) -> q r s w t", r=ROWS, s=2, w=32)
            copy(out=dst[:, lo:hi, s, 0:31, :], in_=src)

        tws = {}

        def turn_w(j):
            tw = psum.tile([P, 512], F32, name="bank")
            view = tw[:].rearrange("q (o t) -> q o t", t=4)
            for t in range(4):
                first = 4 * t + 2 + j
                nc.tensor.matmul(
                    view[:, :, t], lhsT=w_sb[:, first : first + 2033 : 16], rhs=ident[:], start=True, stop=True
                )
            tws[j] = tw

        gw = keep.tile([P, 1024], BF16, name="gw", align_bytes=64)

        def gather_w(copy, j):
            copy(out=gw[:, 512 * j : 512 * j + 512], in_=tws[j][:])

        def w_codes(tile, j):
            return tile[:, 160 * j : 160 * j + 128]

        def w_scales(tile, j):
            return tile[:].bitcast(U8)[:, 640 * j + 512 : 640 * j + 640]

        def quantise_w(j):
            nc.vector.quantize_mx(
                out=w_codes(w_q, j).bitcast(FP8X4), scales=w_scales(w_q, j), in_=gw[:, 512 * j : 512 * j + 512]
            )

        def cross_w(j0, j1):
            c0, c1 = 160 * j0, 160 * j1
            nc.sync.dma_start(out=w_other[0][lower, c0:c1].bitcast(I32), in_=w_q[upper, c0:c1].bitcast(I32))
            nc.sync.dma_start(out=w_other[1][upper, c0:c1].bitcast(I32), in_=w_q[lower, c0:c1].bitcast(I32))

        def stuff_w(j):
            for g, half in ((0, lower), (1, upper)):
                vec(
                    out=w_own[g][half, 128 * j : 128 * j + 128].bitcast(I32),
                    in_=w_q[half, 160 * j : 160 * j + 128].bitcast(I32),
                )

        def keep_warm(count):
            spare = psum.tile([P, 512], F32, name="bank")
            for d in range(count):
                nc.tensor.matmul(spare[:], lhsT=ident[:], rhs=w_sb[:, 0:512], start=True, stop=True)

        def bias_matmul():
            b_col = psum.tile([P, 512], F32, name="bank")
            nc.tensor.matmul(b_col[:, 0:1], lhsT=b_row[:], rhs=ident[:, 0:1], start=True, stop=True)
            return b_col

        def columns(u):
            n, lo, hi = UNITS[u]
            return (0 if lo == 0 else 64 * (lo + 1)), 64 * (hi + 1)

        def quantise(u):
            n = UNITS[u][0]
            c0, c1 = columns(u)
            for a, b in [(c0, c1)] if c0 else [(0, c1 - 64), (c1 - 64, c1)]:
                nc.vector.quantize_mx(
                    out=codes[n][:, 16 + a : 16 + b].bitcast(FP8X4),
                    scales=planes[n][:, 64 + a : 64 + b],
                    in_=grp[n][:, 4 * a : 4 * b],
                )

        def shift_codes(u, move=nc.vector.tensor_copy):
            n = UNITS[u][0]
            c0, c1 = columns(u)
            move(out=codes_r[n][:, c0:c1].bitcast(I32), in_=codes[n][:, 15 + c0 : 15 + c1].bitcast(I32))

        def shift_planes(u):
            n = UNITS[u][0]
            c0, c1 = columns(u)
            vec(out=planes_r[n][:, c0:c1], in_=planes[n][:, 63 + c0 : 63 + c1])

        res = {}
        for n in range(PAIRS):
            for g in range(2):
                res[(n, g)] = keep.tile([P, 1024], F32, name="res%d%d" % (n, g))
        accs = {}

        def passes(u, order):
            n, lo, hi = UNITS[u]
            width = 64 * (hi - lo)
            done = [0, 0]
            for g, j, i in order:
                if done[g] == 0:
                    accs[(u, g)] = psum.tile([P, 512], F32, name="bank")
                done[g] += 1
                if i != g:
                    w_part = w_own[g][:, 128 * j : 128 * j + 128]
                    w_plane = w_scales(w_q, j)
                else:
                    w_part = w_codes(w_other[g], j)
                    w_plane = w_scales(w_other[g], j)
                c0 = (lo + i) * 64
                if j == 1:
                    x_codes = codes[n][:, 16 + c0 : 16 + c0 + width]
                    x_plane = planes[n][:, 64 + c0 : 64 + c0 + width]
                else:
                    x_codes = codes_r[n][:, c0 : c0 + width]
                    x_plane = planes_r[n][:, c0 : c0 + width]
                nc.tensor.matmul_mx(
                    out=accs[(u, g)][:, 0:width],
                    lhsT=w_part.bitcast(FP8X4),
                    lhsT_scale=w_plane,
                    rhs=x_codes.bitcast(FP8X4),
                    rhs_scale=x_plane,
                    start=(done[g] == 1),
                    stop=(done[g] == 4),
                )

        def evacuate(u, g, on_vector=False):
            n, lo, hi = UNITS[u]
            src = accs[(u, g)][:, 0 : 64 * (hi - lo)].rearrange("o (r s z) -> o s r z", s=2, z=32)
            o_v = res[(n, g)][:].rearrange("o (s r z) -> o s r z", s=2, r=16)[:, :, lo:hi, :]
            if on_vector:
                nc.vector.tensor_scalar(out=o_v, in0=src, scalar1=b32[:, 0:1], scalar2=None, op0=ADD)
            else:
                nc.scalar.activation(out=o_v, in_=src, func=IDENT, bias=b32[:, 0:1], scale=1.0)

        def store(u, g):
            n, lo, hi = UNITS[u]
            if n == PAIRS - 1:
                dram = out[2 * n + g].rearrange("o (s r) z -> o s r z", s=2)
                o_v = res[(n, g)][:].rearrange("o (s r z) -> o s r z", s=2, r=16)
                nc.sync.dma_start(out=dram[:, :, lo:hi, :], in_=o_v[:, :, lo:hi, :])
            elif hi == 16:
                nc.sync.dma_start(out=out[2 * n + g].rearrange("o y z -> o (y z)"), in_=res[(n, g)][:])

        corners = ((0, 0), (0, 1), (1, 0), (1, 1))
        own_first = [(g, j, i) for own in (True, False) for j in (1, 0) for g, i in corners if (g != i) == own]
        both = [(g, j, i) for j in (1, 0) for g in (0, 1) for i in (0, 1)]
        in_turn = [(g, j, i) for g in (0, 1) for j in (1, 0) for i in (0, 1)]
        shares = (
            ((act, 1, 4, 9), (vec, 0, 1, 9), (vec, 1, 0, 4)),
            ((act, 1, 9, 16), (act, 0, 11, 17), (vec, 0, 9, 11)),
            ((act, 1, 0, 9), (vec, 0, 1, 9)),
            ((act, 1, 9, 16), (vec, 0, 9, 17)),
            ((act, 1, 2, 9), (vec, 0, 1, 9), (vec, 1, 0, 2)),
            ((act, 1, 11, 16), (vec, 0, 9, 17), (vec, 1, 9, 11)),
            ((act, 1, 2, 9), (vec, 0, 1, 9), (vec, 1, 0, 2)),
            ((act, 1, 11, 13), (vec, 0, 9, 13), (vec, 1, 9, 11)),
            ((act, 1, 13, 15), (vec, 0, 13, 15)),
            ((act, 1, 15, 16), (vec, 0, 15, 17)),
        )

        def regroup_unit(u):
            for copy, s, lo, hi in shares[u]:
                regroup(copy, UNITS[u][0], s, lo, hi)

        vec(out=w_sb[:, 1026:2050], in_=w_sb[:, 0:1024])
        nc.vector.memset(gm[:, :, 0, 0:56], 0)
        nc.vector.memset(gm[:, :, 2 * ROWS - 1, 0:56], 0)
        nc.vector.memset(codes_all[:, :, 0:16].bitcast(I32), 0)
        turn_w(1)
        turn_w(0)
        b_col = bias_matmul()
        keep_warm(2)
        regroup_unit(0)
        gather_w(act, 1)
        gather_w(act, 0)
        act(out=b32[:], in_=b_col[:, 0:1])
        quantise(0)
        quantise_w(1)
        cross_w(1, 2)
        quantise_w(0)
        cross_w(0, 1)
        load(2)
        load(3)
        stuff_w(1)
        shift_codes(0)
        shift_planes(0)
        stuff_w(0)
        regroup_unit(1)
        quantise(1)
        regroup_unit(2)
        shift_codes(1)
        shift_planes(1)
        by_dma = ()
        for u in range(LAST + 1):
            passes(u, own_first if u == 0 else both if u < LAST else in_turn)
            if u + 2 <= LAST:
                quantise(u + 2)
                if u + 2 in by_dma:
                    shift_codes(u + 2, nc.sync.dma_start)
            if u + 3 <= LAST:
                regroup_unit(u + 3)
            if u + 2 <= LAST:
                if u + 2 not in by_dma:
                    shift_codes(u + 2)
                shift_planes(u + 2)
            if u > 0:
                evacuate(u - 1, 1)
                store(u - 1, 1)
            evacuate(u, 0)
            store(u, 0)
        evacuate(LAST, 1, on_vector=True)
        store(LAST, 1)
